import numpy as np
import ml_dtypes


def mxq(x, axis, fmt="e4m3"):
    dtype, down = {"e4m3": (ml_dtypes.float8_e4m3fn, 7), "e5m2": (ml_dtypes.float8_e5m2, 14)}[fmt]
    v = np.moveaxis(np.asarray(x, np.float32).astype(ml_dtypes.bfloat16).astype(np.float64), axis, -1)
    blocks = v.reshape(v.shape[:-1] + (-1, 32))
    amax = np.abs(blocks).max(-1, keepdims=True)
    byte = np.maximum(np.where(amax > 0, np.frexp(amax)[1] - 1 + 127, 0) - down, 1)
    scale = np.exp2(byte - 127.0)
    codes = (blocks / scale).astype(np.float32).astype(dtype).astype(np.float64)
    return np.moveaxis((codes * scale).reshape(v.shape), -1, axis)


WIDE = False


def mx_kscale(k):
    if not WIDE:
        return np.ones(k)
    levels = np.array([10, -10, 5, -5, 0])
    a = np.random.permutation(np.resize(levels, k // 512 * 4)).reshape(k // 512, 4)
    idx = np.arange(k)
    return np.exp2(a[idx // 512, idx % 128 // 32])


BF16 = ml_dtypes.bfloat16


def bf(x):
    return np.asarray(x, np.float32).astype(BF16)


def f64(x):
    return np.asarray(x).astype(np.float64)


B, D_IN, D_H = 2048, 256, 256
K = D_IN + D_H
PROJ_EPS = 1e-5


def _norm(x):
    return np.linalg.norm(x, axis=-1, keepdims=True)


def logmap0(x):
    n = _norm(x)
    ns = np.where(n == 0, 0.5, n)
    return np.where(n == 0, np.zeros_like(x), np.arctanh(ns) * x / ns)


def expmap0(v):
    n = _norm(v)
    ns = np.where(n == 0, 1.0, n)
    return np.where(n == 0, np.zeros_like(v), np.tanh(ns) * v / ns)


def proj(x):
    n = _norm(x)
    maxnorm = 1.0 - PROJ_EPS
    ns = np.where(n == 0, 1.0, n)
    return np.where(n > maxnorm, x / ns * maxnorm, x)


def sigmoid(v):
    return 1.0 / (1.0 + np.exp(-v))


def ball(g):
    return g / _norm(g) * np.random.uniform(0.5, 0.9, (g.shape[0], 1))


def setup_inputs():
    s = mx_kscale(K)[:D_IN]
    c = np.sqrt(np.mean(s * s))
    u = np.concatenate([c / s, np.ones(D_H)])[:, None]
    return {"x": bf(ball(np.random.standard_normal((B, D_IN)) * s)),
            "h": bf(ball(np.random.standard_normal((B, D_H)))),
            "Wr": bf(np.random.standard_normal((K, D_H)) * 0.75 * u),
            "br": bf(np.random.standard_normal(D_H) * 0.5),
            "Wz": bf(np.random.standard_normal((K, D_H)) * 0.75 * u),
            "bz": bf(np.random.standard_normal(D_H) * 0.3 - 0.5 * np.log(D_H)),
            "Wh": bf(np.random.standard_normal((K, D_H)) * 0.7 * u),
            "bh": bf(np.random.standard_normal(D_H) * 0.3)}


def reference(x, h, Wr, br, Wz, bz, Wh, bh):
    x_tan = logmap0(f64(x))
    h_tan = logmap0(f64(h))
    xh = mxq(np.concatenate([x_tan, h_tan], axis=1), 1, "e4m3")
    r = sigmoid((xh @ mxq(f64(Wr), 0, "e4m3")) + f64(br))
    z = sigmoid((xh @ mxq(f64(Wz), 0, "e4m3")) + f64(bz))
    xh_reset = mxq(np.concatenate([x_tan, r * h_tan], axis=1), 1, "e4m3")
    h_tilde = np.tanh((xh_reset @ mxq(f64(Wh), 0, "e4m3")) + f64(bh))
    h_new_tan = (1.0 - z) * h_tan + z * h_tilde
    return proj(expmap0(h_new_tan))

@@ -1,0 +1,372 @@
+from contextlib import ExitStack
+
+import concourse.mybir as mybir
+from concourse.masks import make_identity
+
+F32 = mybir.dt.float32
+BF16 = mybir.dt.bfloat16
+I32 = mybir.dt.int32
+U32 = mybir.dt.uint32
+U8 = mybir.dt.uint8
+FP8X4 = mybir.dt.float8_e4m3fn_x4
+ACT = mybir.ActivationFunctionType
+ALU = mybir.AluOpType
+
+P = 128
+HALF = 64
+PACK = 4
+BATCH = 2048
+D = 256
+ROWS = BATCH // P
+CHUNKS = 4
+CHUNK_ROWS = ROWS // CHUNKS
+CHUNK_PAIRS = CHUNK_ROWS // 2
+CHUNK_COLS = CHUNK_PAIRS * P
+GATES = 3
+R, Z, N = 0, 1, 2
+TINY = 1e-30
+MAX_NORM = 1.0 - 1e-5
+
+FLOPS = 3 * 2 * BATCH * (2 * D) * D
+
+
+def tile_hyperbolicgru_kernel(tc, x, h, Wr, br, Wz, bz, Wh, bh, out):
+    nc = tc.nc
+    with ExitStack() as ctx:
+        keep = ctx.enter_context(tc.tile_pool(name="keep", bufs=1))
+        work = ctx.enter_context(tc.tile_pool(name="work", bufs=2))
+        turn_psum = ctx.enter_context(tc.psum_pool(name="turn_psum", bufs=4))
+        gate_psum = ctx.enter_context(tc.psum_pool(name="gate_psum", bufs=4))
+        ctx.enter_context(tc.manual_schedule())
+
+        def chunk_rows(k):
+            return slice(k * CHUNK_ROWS, (k + 1) * CHUNK_ROWS)
+
+        x_rows = x.rearrange("(c r) f -> c (r f)", r=ROWS)
+        h_rows = h.rearrange("(c r) f -> c (r f)", r=ROWS)
+        out_rows = out.rearrange("(c r) f -> c (r f)", r=ROWS)
+        x_sb = keep.tile([P, ROWS * D], BF16, name="x_sb")
+        h_sb = keep.tile([P, ROWS * D], BF16, name="h_sb")
+        w_raw = keep.tile([P, GATES, 2, PACK, D], BF16, name="w_raw")
+        bias_bf = keep.tile([P, GATES, 16], BF16, name="bias_bf")
+
+        def load_rows(k):
+            cols = slice(k * CHUNK_ROWS * D, (k + 1) * CHUNK_ROWS * D)
+            nc.sync.dma_start(out=x_sb[:, cols], in_=x_rows[:, cols])
+            nc.sync.dma_start(out=h_sb[:, cols], in_=h_rows[:, cols])
+
+        def load_weights(g, w):
+            w_view = w.rearrange("(s q j) n -> q s j n", s=2, j=PACK)
+            for half in range(2):
+                nc.sync.dma_start(out=w_raw[half * HALF : (half + 1) * HALF, g], in_=w_view)
+
+        def load_bias(g, b):
+            b_view = b.rearrange("(q t) -> q t", t=PACK)
+            for half in range(2):
+                nc.sync.dma_start(out=bias_bf[half * HALF : (half + 1) * HALF, g, 0:PACK], in_=b_view)
+
+        load_rows(0)
+        load_weights(R, Wr)
+        load_rows(1)
+        load_weights(Z, Wz)
+        load_rows(2)
+        load_weights(N, Wh)
+        load_rows(3)
+        with nc.allow_non_contiguous_dma(reason="four bias values to a partition"):
+            load_bias(R, br)
+            load_bias(Z, bz)
+            load_bias(N, bh)
+
+        ident = keep.tile([P, P], F32, name="ident")
+        make_identity(nc, ident[:])
+        one_half = keep.tile([P, CHUNK_ROWS], F32, name="one_half")
+        nc.gpsimd.memset(one_half[:], 0.5)
+        warm = keep.tile([P, 2], F32, name="warm")
+        nc.vector.memset(warm[:, 0:1], 1.0)
+        nc.scalar.activation(out=warm[:, 1:2], in_=warm[:, 0:1], func=ACT.Ln)
+
+        w_codes = keep.tile([P, GATES, 2 * PACK, P], U32, name="w_codes", align_bytes=64)
+        w_scales = keep.tile([P, GATES, 2 * PACK, P], U8, name="w_scales", align_bytes=64)
+        nc.vector.memset(w_codes[:].bitcast(I32), 0)
+        nc.vector.memset(w_scales[:].bitcast(I32), 0)
+        w_grouped = keep.tile([P, GATES, 2, PACK, HALF, PACK], BF16, name="w_grouped", align_bytes=64)
+        block_codes = keep.tile([P, GATES, 2 * PACK, HALF], U32, name="block_codes", align_bytes=64)
+        block_scales = keep.tile([P, GATES, 2 * PACK, HALF], U8, name="block_scales", align_bytes=64)
+
+        def prepare_weights(g):
+            for s in range(2):
+                nc.vector.tensor_copy(
+                    out=w_grouped[:, g, s],
+                    in_=w_raw[:, g, s].rearrange("p j (m t) -> p t m j", t=PACK),
+                )
+            nc.vector.quantize_mx(
+                out=block_codes[:, g].rearrange("p a m -> p (a m)").bitcast(FP8X4),
+                scales=block_scales[:, g].rearrange("p a m -> p (a m)"),
+                in_=w_grouped[:, g].rearrange("p s t m j -> p (s t m j)"),
+            )
+            for half in range(2):
+                rows = slice(half * HALF, (half + 1) * HALF)
+                cols = slice(half * HALF, (half + 1) * HALF)
+                nc.vector.tensor_copy(
+                    out=w_codes[rows, g, :, cols].bitcast(I32), in_=block_codes[rows, g].bitcast(I32)
+                )
+                nc.vector.tensor_copy(
+                    out=w_scales[rows, g, :, cols].bitcast(I32), in_=block_scales[rows, g].bitcast(I32)
+                )
+
+        squares = keep.tile([P, 2, ROWS * D], BF16, name="squares")
+        sumsq = keep.tile([P, 2, ROWS], F32, name="sumsq")
+        norm = keep.tile([P, 2, ROWS], F32, name="norm")
+        inv_norm = keep.tile([P, 2, ROWS], F32, name="inv_norm")
+        ln_plus = keep.tile([P, 2, ROWS], F32, name="ln_plus")
+        ln_minus = keep.tile([P, 2, ROWS], F32, name="ln_minus")
+        ln_diff = keep.tile([P, 2, ROWS], F32, name="ln_diff")
+        factor = keep.tile([P, 2, ROWS], F32, name="factor")
+
+        def norms(k):
+            rows = chunk_rows(k)
+            for o, src in enumerate((x_sb, h_sb)):
+                for r in range(k * CHUNK_ROWS, (k + 1) * CHUNK_ROWS):
+                    nc.scalar.activation(
+                        out=squares[:, o, r * D : (r + 1) * D],
+                        in_=src[:, r * D : (r + 1) * D],
+                        func=ACT.Square,
+                        accum_out=sumsq[:, o, r : r + 1],
+                    )
+                nc.gpsimd.tensor_tensor(out=norm[:, o, rows], in0=sumsq[:, o, rows], in1=one_half[:], op=ALU.pow)
+
+        def factors(k):
+            rows = chunk_rows(k)
+            nc.scalar.activation(out=ln_plus[:, :, rows], in_=norm[:, :, rows], func=ACT.Ln, bias=1.0, scale=1.0)
+            nc.scalar.activation(out=ln_minus[:, :, rows], in_=norm[:, :, rows], func=ACT.Ln, bias=1.0, scale=-1.0)
+            nc.vector.tensor_scalar_max(out=inv_norm[:, :, rows], in0=norm[:, :, rows], scalar1=TINY)
+            nc.vector.reciprocal(out=inv_norm[:, :, rows], in_=inv_norm[:, :, rows])
+            nc.vector.tensor_tensor(out=ln_diff[:, :, rows], in0=ln_plus[:, :, rows], in1=ln_minus[:, :, rows], op=ALU.subtract)
+            nc.vector.scalar_tensor_tensor(
+                out=factor[:, :, rows], in0=ln_diff[:, :, rows], scalar=0.5, in1=inv_norm[:, :, rows],
+                op0=ALU.mult, op1=ALU.mult,
+            )
+
+        tiles = {}
+
+        x_words = x_sb[:].bitcast(F32).rearrange("c (g p u) -> c g u p", p=P, u=2)
+        h_words = h_sb[:].bitcast(F32).rearrange("c (g p u) -> c g u p", p=P, u=2)
+
+        def spread(k):
+            repeated = work.tile([P, 2, CHUNK_ROWS, HALF], F32, name="repeated")
+            nc.vector.tensor_copy(
+                out=repeated[:],
+                in_=factor[:, :, chunk_rows(k)].unsqueeze(3).to_broadcast([P, 2, CHUNK_ROWS, HALF]),
+            )
+            factor_ps = turn_psum.tile([P, 2, CHUNK_COLS], F32, name="factor_ps", tag="turn")
+            for o in range(2):
+                for a in range(CHUNK_PAIRS):
+                    nc.tensor.transpose(
+                        out=factor_ps[:, o, a * P : (a + 1) * P],
+                        in_=repeated[:, o, 2 * a : 2 * a + 2, :].rearrange("c r q -> c (r q)"),
+                        identity=ident[:],
+                    )
+            factor_t = work.tile([P, 2, CHUNK_COLS], F32, name="factor_t")
+            nc.scalar.copy(out=factor_t[:], in_=factor_ps[:])
+            tiles["factor_t", k] = factor_t
+
+        def turn(k):
+            for name, words in (("x_ps", x_words), ("h_ps", h_words)):
+                words_ps = turn_psum.tile([P, 2, CHUNK_COLS], F32, name="words_ps", tag="turn")
+                for a in range(CHUNK_PAIRS):
+                    for u in range(2):
+                        nc.tensor.transpose(
+                            out=words_ps[:, u, a * P : (a + 1) * P],
+                            in_=words[:, k * CHUNK_PAIRS + a, u, :],
+                            identity=ident[:],
+                        )
+                tiles[name, k] = words_ps
+
+        def logmap(k):
+            factor_t = tiles["factor_t", k]
+            xh_grouped = work.tile([P, 2, CHUNK_COLS, PACK], BF16, name="xh_grouped", align_bytes=64)
+            nc.vector.tensor_tensor(
+                out=xh_grouped[:, 0].rearrange("p c (u e) -> p c u e", u=2),
+                in0=tiles["x_ps", k][:].bitcast(BF16).rearrange("p u (c e) -> p c u e", e=2),
+                in1=factor_t[:, 0, :].unsqueeze(2).unsqueeze(3).to_broadcast([P, CHUNK_COLS, 2, 2]),
+                op=ALU.mult,
+            )
+            h_tan = work.tile([P, PACK, CHUNK_COLS], F32, name="h_tan")
+            nc.vector.tensor_tensor(
+                out=h_tan[:].rearrange("p (u e) c -> p u e c", u=2),
+                in0=tiles["h_ps", k][:].bitcast(BF16).rearrange("p u (c e) -> p u e c", e=2),
+                in1=factor_t[:, 1, :].unsqueeze(1).unsqueeze(2).to_broadcast([P, 2, 2, CHUNK_COLS]),
+                op=ALU.mult,
+            )
+            nc.scalar.copy(out=xh_grouped[:, 1], in_=h_tan[:].rearrange("p t c -> p c t"))
+            tiles["xh_grouped", k] = xh_grouped
+            tiles["h_tan", k] = h_tan
+
+        def quantise_xh(k):
+            xh_codes = work.tile([P, 2, CHUNK_COLS], U32, name="xh_codes", align_bytes=64)
+            xh_scales = work.tile([P, 2, CHUNK_COLS], U8, name="xh_scales", align_bytes=64)
+            nc.vector.quantize_mx(
+                out=xh_codes[:].rearrange("p o c -> p (o c)").bitcast(FP8X4),
+                scales=xh_scales[:].rearrange("p o c -> p (o c)"),
+                in_=tiles["xh_grouped", k][:].rearrange("p o c t -> p (o c t)"),
+            )
+            tiles["x_mx", k] = (xh_codes[:, 0, :], xh_scales[:, 0, :])
+            tiles["h_mx", k] = (xh_codes[:, 1, :], xh_scales[:, 1, :])
+
+        bias = keep.tile([P, GATES, PACK], F32, name="bias")
+
+        def gate(g, func, operands, result):
+            for t_pair in range(2):
+                acc = gate_psum.tile([P, 2, CHUNK_COLS], F32, name="acc")
+                for i in range(2):
+                    t = 2 * t_pair + i
+                    for s, (codes, scales) in enumerate(operands):
+                        nc.tensor.matmul_mx(
+                            out=acc[:, i, :],
+                            lhsT=w_codes[:, g, s * PACK + t, :].bitcast(FP8X4),
+                            lhsT_scale=w_scales[:, g, s * PACK + t, :],
+                            rhs=codes.bitcast(FP8X4),
+                            rhs_scale=scales,
+                            start=(s == 0),
+                            stop=(s == 1),
+                        )
+                for i in range(2):
+                    t = 2 * t_pair + i
+                    nc.scalar.activation(
+                        out=result[:, t, :], in_=acc[:, i, :], func=func, bias=bias[:, g, t : t + 1], scale=1.0
+                    )
+
+        def gate_r(k):
+            r_t = work.tile([P, PACK, CHUNK_COLS], F32, name="r_t")
+            gate(R, ACT.Sigmoid, (tiles["x_mx", k], tiles["h_mx", k]), r_t)
+            tiles["r_t", k] = r_t
+
+        def gate_z(k):
+            z_t = work.tile([P, PACK, CHUNK_COLS], F32, name="z_t")
+            gate(Z, ACT.Sigmoid, (tiles["x_mx", k], tiles["h_mx", k]), z_t)
+            tiles["z_t", k] = z_t
+
+        def reset(k):
+            rh_grouped = work.tile([P, CHUNK_COLS, PACK], BF16, name="rh_grouped", align_bytes=64)
+            nc.vector.tensor_tensor(
+                out=rh_grouped[:],
+                in0=tiles["r_t", k][:].rearrange("p t c -> p c t"),
+                in1=tiles["h_tan", k][:].rearrange("p t c -> p c t"),
+                op=ALU.mult,
+            )
+            rh_codes = work.tile([P, CHUNK_COLS], U32, name="rh_codes", align_bytes=64)
+            rh_scales = work.tile([P, CHUNK_COLS], U8, name="rh_scales", align_bytes=64)
+            nc.vector.quantize_mx(
+                out=rh_codes[:].bitcast(FP8X4),
+                scales=rh_scales[:],
+                in_=rh_grouped[:].rearrange("p c t -> p (c t)"),
+            )
+            tiles["rh_mx", k] = (rh_codes[:], rh_scales[:])
+
+        def gate_n(k):
+            n_t = work.tile([P, PACK, CHUNK_COLS], F32, name="n_t")
+            gate(N, ACT.Tanh, (tiles["x_mx", k], tiles["rh_mx", k]), n_t)
+            tiles["n_t", k] = n_t
+
+        def mix(k):
+            n_t = tiles["n_t", k]
+            move_t = work.tile([P, PACK, CHUNK_COLS], F32, name="move_t")
+            nc.vector.tensor_tensor(out=n_t[:], in0=n_t[:], in1=tiles["h_tan", k][:], op=ALU.subtract)
+            nc.vector.tensor_tensor(out=move_t[:], in0=tiles["z_t", k][:], in1=n_t[:], op=ALU.mult)
+            tiles["move_t", k] = move_t
+
+        def turn_back(k):
+            for a in range(CHUNK_PAIRS):
+                move_ps = turn_psum.tile([P, PACK, P], F32, name="move_ps", tag="turn")
+                for t in range(PACK):
+                    nc.tensor.transpose(
+                        out=move_ps[:, t, :], in_=tiles["move_t", k][:, t, a * P : (a + 1) * P], identity=ident[:]
+                    )
+                tiles["move_ps", k, a] = move_ps
+
+        v_sumsq = keep.tile([P, ROWS], F32, name="v_sumsq")
+        v_norm = keep.tile([P, ROWS], F32, name="v_norm")
+        v_inv = keep.tile([P, ROWS], F32, name="v_inv")
+        v_tanh = keep.tile([P, ROWS], F32, name="v_tanh")
+        v_factor = keep.tile([P, ROWS], F32, name="v_factor")
+
+        def new_tangent(k):
+            v = work.tile([P, CHUNK_ROWS, D], F32, name="v")
+            for i in range(CHUNK_ROWS):
+                r = k * CHUNK_ROWS + i
+                half = i % 2
+                nc.vector.scalar_tensor_tensor(
+                    out=v[:, i, :].rearrange("c (q t) -> c q t", t=PACK),
+                    in0=h_sb[:, r * D : (r + 1) * D].rearrange("c (q t) -> c q t", t=PACK),
+                    scalar=factor[:, 1, r : r + 1],
+                    in1=tiles["move_ps", k, i // 2][:, :, half * HALF : (half + 1) * HALF].rearrange("c t q -> c q t"),
+                    op0=ALU.mult,
+                    op1=ALU.add,
+                )
+                nc.scalar.activation(
+                    out=squares[:, 0, r * D : (r + 1) * D], in_=v[:, i, :], func=ACT.Square,
+                    accum_out=v_sumsq[:, r : r + 1],
+                )
+            nc.gpsimd.tensor_tensor(out=v_norm[:, chunk_rows(k)], in0=v_sumsq[:, chunk_rows(k)], in1=one_half[:], op=ALU.pow)
+            tiles["v", k] = v
+
+        def tanh_of_norm(k):
+            nc.scalar.activation(out=v_tanh[:, chunk_rows(k)], in_=v_norm[:, chunk_rows(k)], func=ACT.Tanh)
+
+        def finish(k):
+            rows = chunk_rows(k)
+            nc.vector.tensor_scalar_max(out=v_inv[:, rows], in0=v_norm[:, rows], scalar1=TINY)
+            nc.vector.reciprocal(out=v_inv[:, rows], in_=v_inv[:, rows])
+            nc.vector.scalar_tensor_tensor(
+                out=v_factor[:, rows], in0=v_tanh[:, rows], scalar=MAX_NORM, in1=v_inv[:, rows],
+                op0=ALU.min, op1=ALU.mult,
+            )
+            result = work.tile([P, CHUNK_ROWS, D], F32, name="result")
+            for i in range(CHUNK_ROWS):
+                r = k * CHUNK_ROWS + i
+                nc.vector.tensor_scalar_mul(
+                    out=result[:, i, :], in0=tiles["v", k][:, i, :], scalar1=v_factor[:, r : r + 1]
+                )
+            nc.sync.dma_start(
+                out=out_rows[:, k * CHUNK_ROWS * D : (k + 1) * CHUNK_ROWS * D],
+                in_=result[:].rearrange("c r f -> c (r f)"),
+            )
+
+        norms(0)
+        prepare_weights(R)
+        norms(1)
+        factors(0)
+        norms(2)
+        spread(0)
+        turn(0)
+        prepare_weights(Z)
+        factors(1)
+        norms(3)
+        logmap(0)
+        spread(1)
+        turn(1)
+        factors(2)
+        quantise_xh(0)
+        nc.vector.tensor_copy(out=bias[:], in_=bias_bf[:, :, 0:PACK])
+        prepare_weights(N)
+        factors(3)
+        nc.scalar.activation(out=warm[:, 1:2], in_=warm[:, 0:1], func=ACT.Sigmoid)
+
+        def staged(stage, k):
+            if 0 <= k < CHUNKS:
+                stage(k)
+
+        for i in range(CHUNKS + 2):
+            staged(gate_r, i)
+            staged(tanh_of_norm, i - 2)
+            staged(gate_z, i)
+            staged(mix, i - 1)
+            staged(turn_back, i - 1)
+            staged(finish, i - 2)
+            staged(logmap, i + 1)
+            staged(spread, i + 2)
+            staged(reset, i)
+            staged(gate_n, i)
+            staged(new_tangent, i - 1)
+            staged(turn, i + 2)
+            staged(quantise_xh, i + 1)

@@ -35,6 +35,7 @@ def tile_hyperbolicgru_kernel(tc, x, h, Wr, br, Wz, bz, Wh, bh, out):
     with ExitStack() as ctx:
         keep = ctx.enter_context(tc.tile_pool(name="keep", bufs=1))
         work = ctx.enter_context(tc.tile_pool(name="work", bufs=2))
+        held = ctx.enter_context(tc.tile_pool(name="held", bufs=CHUNKS))
         turn_psum = ctx.enter_context(tc.psum_pool(name="turn_psum", bufs=4))
         gate_psum = ctx.enter_context(tc.psum_pool(name="gate_psum", bufs=4))
         ctx.enter_context(tc.manual_schedule())
@@ -185,13 +186,7 @@ def tile_hyperbolicgru_kernel(tc, x, h, Wr, br, Wz, bz, Wh, bh, out):
         def logmap(k):
             factor_t = tiles["factor_t", k]
             xh_grouped = work.tile([P, 2, CHUNK_COLS, PACK], BF16, name="xh_grouped", align_bytes=64)
-            nc.vector.tensor_tensor(
-                out=xh_grouped[:, 0].rearrange("p c (u e) -> p c u e", u=2),
-                in0=tiles["x_ps", k][:].bitcast(BF16).rearrange("p u (c e) -> p c u e", e=2),
-                in1=factor_t[:, 0, :].unsqueeze(2).unsqueeze(3).to_broadcast([P, CHUNK_COLS, 2, 2]),
-                op=ALU.mult,
-            )
-            h_tan = work.tile([P, PACK, CHUNK_COLS], F32, name="h_tan")
+            h_tan = held.tile([P, PACK, CHUNK_COLS], F32, name="h_tan")
             nc.vector.tensor_tensor(
                 out=h_tan[:].rearrange("p (u e) c -> p u e c", u=2),
                 in0=tiles["h_ps", k][:].bitcast(BF16).rearrange("p u (c e) -> p u e c", e=2),
@@ -199,12 +194,18 @@ def tile_hyperbolicgru_kernel(tc, x, h, Wr, br, Wz, bz, Wh, bh, out):
                 op=ALU.mult,
             )
             nc.scalar.copy(out=xh_grouped[:, 1], in_=h_tan[:].rearrange("p t c -> p c t"))
+            nc.vector.tensor_tensor(
+                out=xh_grouped[:, 0].rearrange("p c (u e) -> p c u e", u=2),
+                in0=tiles["x_ps", k][:].bitcast(BF16).rearrange("p u (c e) -> p c u e", e=2),
+                in1=factor_t[:, 0, :].unsqueeze(2).unsqueeze(3).to_broadcast([P, CHUNK_COLS, 2, 2]),
+                op=ALU.mult,
+            )
             tiles["xh_grouped", k] = xh_grouped
             tiles["h_tan", k] = h_tan
 
         def quantise_xh(k):
-            xh_codes = work.tile([P, 2, CHUNK_COLS], U32, name="xh_codes", align_bytes=64)
-            xh_scales = work.tile([P, 2, CHUNK_COLS], U8, name="xh_scales", align_bytes=64)
+            xh_codes = held.tile([P, 2, CHUNK_COLS], U32, name="xh_codes", align_bytes=64)
+            xh_scales = held.tile([P, 2, CHUNK_COLS], U8, name="xh_scales", align_bytes=64)
             nc.vector.quantize_mx(
                 out=xh_codes[:].rearrange("p o c -> p (o c)").bitcast(FP8X4),
                 scales=xh_scales[:].rearrange("p o c -> p (o c)"),
@@ -212,8 +213,6 @@ def tile_hyperbolicgru_kernel(tc, x, h, Wr, br, Wz, bz, Wh, bh, out):
             )
             tiles["x_mx", k] = (xh_codes[:, 0, :], xh_scales[:, 0, :])
             tiles["h_mx", k] = (xh_codes[:, 1, :], xh_scales[:, 1, :])
-
-        bias = keep.tile([P, GATES, PACK], F32, name="bias")
 
         def gate(g, func, operands, result):
             for t_pair in range(2):
@@ -233,16 +232,16 @@ def tile_hyperbolicgru_kernel(tc, x, h, Wr, br, Wz, bz, Wh, bh, out):
                 for i in range(2):
                     t = 2 * t_pair + i
                     nc.scalar.activation(
-                        out=result[:, t, :], in_=acc[:, i, :], func=func, bias=bias[:, g, t : t + 1], scale=1.0
+                        out=result[:, t, :], in_=acc[:, i, :], func=func, bias=bias_bf[:, g, t : t + 1], scale=1.0
                     )
 
         def gate_r(k):
-            r_t = work.tile([P, PACK, CHUNK_COLS], F32, name="r_t")
+            r_t = held.tile([P, PACK, CHUNK_COLS], F32, name="r_t")
             gate(R, ACT.Sigmoid, (tiles["x_mx", k], tiles["h_mx", k]), r_t)
             tiles["r_t", k] = r_t
 
         def gate_z(k):
-            z_t = work.tile([P, PACK, CHUNK_COLS], F32, name="z_t")
+            z_t = held.tile([P, PACK, CHUNK_COLS], F32, name="z_t")
             gate(Z, ACT.Sigmoid, (tiles["x_mx", k], tiles["h_mx", k]), z_t)
             tiles["z_t", k] = z_t
 
@@ -264,16 +263,16 @@ def tile_hyperbolicgru_kernel(tc, x, h, Wr, br, Wz, bz, Wh, bh, out):
             tiles["rh_mx", k] = (rh_codes[:], rh_scales[:])
 
         def gate_n(k):
-            n_t = work.tile([P, PACK, CHUNK_COLS], F32, name="n_t")
+            n_t = held.tile([P, PACK, CHUNK_COLS], F32, name="n_t")
             gate(N, ACT.Tanh, (tiles["x_mx", k], tiles["rh_mx", k]), n_t)
             tiles["n_t", k] = n_t
 
         def mix(k):
             n_t = tiles["n_t", k]
-            move_t = work.tile([P, PACK, CHUNK_COLS], F32, name="move_t")
+            z_t = tiles["z_t", k]
             nc.vector.tensor_tensor(out=n_t[:], in0=n_t[:], in1=tiles["h_tan", k][:], op=ALU.subtract)
-            nc.vector.tensor_tensor(out=move_t[:], in0=tiles["z_t", k][:], in1=n_t[:], op=ALU.mult)
-            tiles["move_t", k] = move_t
+            nc.vector.tensor_tensor(out=z_t[:], in0=z_t[:], in1=n_t[:], op=ALU.mult)
+            tiles["move_t", k] = z_t
 
         def turn_back(k):
             for a in range(CHUNK_PAIRS):
@@ -291,7 +290,7 @@ def tile_hyperbolicgru_kernel(tc, x, h, Wr, br, Wz, bz, Wh, bh, out):
         v_factor = keep.tile([P, ROWS], F32, name="v_factor")
 
         def new_tangent(k):
-            v = work.tile([P, CHUNK_ROWS, D], F32, name="v")
+            v = held.tile([P, CHUNK_ROWS, D], F32, name="v")
             for i in range(CHUNK_ROWS):
                 r = k * CHUNK_ROWS + i
                 half = i % 2
@@ -321,52 +320,42 @@ def tile_hyperbolicgru_kernel(tc, x, h, Wr, br, Wz, bz, Wh, bh, out):
                 out=v_factor[:, rows], in0=v_tanh[:, rows], scalar=MAX_NORM, in1=v_inv[:, rows],
                 op0=ALU.min, op1=ALU.mult,
             )
-            result = work.tile([P, CHUNK_ROWS, D], F32, name="result")
-            for i in range(CHUNK_ROWS):
-                r = k * CHUNK_ROWS + i
-                nc.vector.tensor_scalar_mul(
-                    out=result[:, i, :], in0=tiles["v", k][:, i, :], scalar1=v_factor[:, r : r + 1]
+            v = tiles["v", k]
+            for a in range(CHUNK_PAIRS):
+                r = k * CHUNK_ROWS + 2 * a
+                nc.scalar.activation(
+                    out=v[:, 2 * a, :], in_=v[:, 2 * a, :], func=ACT.Copy, scale=v_factor[:, r : r + 1]
                 )
-            nc.sync.dma_start(
-                out=out_rows[:, k * CHUNK_ROWS * D : (k + 1) * CHUNK_ROWS * D],
-                in_=result[:].rearrange("c r f -> c (r f)"),
-            )
+                nc.vector.tensor_scalar_mul(
+                    out=v[:, 2 * a + 1, :], in0=v[:, 2 * a + 1, :], scalar1=v_factor[:, r + 1 : r + 2]
+                )
+                nc.sync.dma_start(
+                    out=out_rows[:, r * D : (r + 2) * D],
+                    in_=v[:, 2 * a : 2 * a + 2, :].rearrange("c r f -> c (r f)"),
+                )
 
-        norms(0)
-        prepare_weights(R)
-        norms(1)
-        factors(0)
-        norms(2)
-        spread(0)
-        turn(0)
-        prepare_weights(Z)
-        factors(1)
-        norms(3)
-        logmap(0)
-        spread(1)
-        turn(1)
-        factors(2)
-        quantise_xh(0)
-        nc.vector.tensor_copy(out=bias[:], in_=bias_bf[:, :, 0:PACK])
-        prepare_weights(N)
-        factors(3)
-        nc.scalar.activation(out=warm[:, 1:2], in_=warm[:, 0:1], func=ACT.Sigmoid)
-
-        def staged(stage, k):
-            if 0 <= k < CHUNKS:
+        def staged(stage, k, count=CHUNKS):
+            if 0 <= k < count:
                 stage(k)
 
-        for i in range(CHUNKS + 2):
-            staged(gate_r, i)
-            staged(tanh_of_norm, i - 2)
-            staged(gate_z, i)
-            staged(mix, i - 1)
-            staged(turn_back, i - 1)
-            staged(finish, i - 2)
-            staged(logmap, i + 1)
-            staged(spread, i + 2)
-            staged(reset, i)
-            staged(gate_n, i)
-            staged(new_tangent, i - 1)
-            staged(turn, i + 2)
-            staged(quantise_xh, i + 1)
+        for j in range(-5, CHUNKS + 1):
+            staged(norms, j + 5)
+            staged(prepare_weights, j + 5, GATES)
+            staged(gate_r, j - 1)
+            staged(logmap, j)
+            staged(factors, j + 3)
+            staged(spread, j + 2)
+            staged(turn, j + 1)
+            staged(quantise_xh, j)
+
+        for k in range(CHUNKS):
+            reset(k)
+            gate_z(k)
+            gate_n(k)
+
+        for k in range(CHUNKS + 4):
+            staged(mix, k)
+            staged(new_tangent, k - 2)
+            staged(turn_back, k)
+            staged(tanh_of_norm, k - 3)
+            staged(finish, k - 4)

@@ -339,23 +339,24 @@ def tile_hyperbolicgru_kernel(tc, x, h, Wr, br, Wz, bz, Wh, bh, out):
                 stage(k)
 
         for j in range(-5, CHUNKS + 1):
-            staged(norms, j + 5)
-            staged(prepare_weights, j + 5, GATES)
-            staged(gate_r, j - 1)
             staged(logmap, j)
+            staged(gate_r, j - 1)
             staged(factors, j + 3)
-            staged(spread, j + 2)
+            staged(norms, j + 5)
             staged(turn, j + 1)
+            staged(spread, j + 2)
+            staged(prepare_weights, j + 4, GATES)
             staged(quantise_xh, j)
 
+        reset(0)
         for k in range(CHUNKS):
-            reset(k)
-            gate_z(k)
             gate_n(k)
+            gate_z(k)
+            staged(reset, k + 1)
 
-        for k in range(CHUNKS + 4):
+        for k in range(CHUNKS + 5):
             staged(mix, k)
             staged(new_tangent, k - 2)
+            staged(tanh_of_norm, k - 4)
             staged(turn_back, k)
-            staged(tanh_of_norm, k - 3)
-            staged(finish, k - 4)
+            staged(finish, k - 5)

@@ -43,13 +43,16 @@ def tile_hyperbolicgru_kernel(tc, x, h, Wr, br, Wz, bz, Wh, bh, out):
         def chunk_rows(k):
             return slice(k * CHUNK_ROWS, (k + 1) * CHUNK_ROWS)
 
+        def halves():
+            return (slice(0, HALF), slice(HALF, P))
+
         x_rows = x.rearrange("(c r) f -> c (r f)", r=ROWS)
         h_rows = h.rearrange("(c r) f -> c (r f)", r=ROWS)
         out_rows = out.rearrange("(c r) f -> c (r f)", r=ROWS)
         x_sb = keep.tile([P, ROWS * D], BF16, name="x_sb")
         h_sb = keep.tile([P, ROWS * D], BF16, name="h_sb")
         w_raw = keep.tile([P, GATES, 2, PACK, D], BF16, name="w_raw")
-        bias_bf = keep.tile([P, GATES, 16], BF16, name="bias_bf")
+        bias = keep.tile([P, GATES, 16], BF16, name="bias")
 
         def load_rows(k):
             cols = slice(k * CHUNK_ROWS * D, (k + 1) * CHUNK_ROWS * D)
@@ -58,13 +61,13 @@ def tile_hyperbolicgru_kernel(tc, x, h, Wr, br, Wz, bz, Wh, bh, out):
 
         def load_weights(g, w):
             w_view = w.rearrange("(s q j) n -> q s j n", s=2, j=PACK)
-            for half in range(2):
-                nc.sync.dma_start(out=w_raw[half * HALF : (half + 1) * HALF, g], in_=w_view)
+            for rows in halves():
+                nc.sync.dma_start(out=w_raw[rows, g], in_=w_view)
 
         def load_bias(g, b):
             b_view = b.rearrange("(q t) -> q t", t=PACK)
-            for half in range(2):
-                nc.sync.dma_start(out=bias_bf[half * HALF : (half + 1) * HALF, g, 0:PACK], in_=b_view)
+            for rows in halves():
+                nc.sync.dma_start(out=bias[rows, g, 0:PACK], in_=b_view)
 
         load_rows(0)
         load_weights(R, Wr)
@@ -94,29 +97,32 @@ def tile_hyperbolicgru_kernel(tc, x, h, Wr, br, Wz, bz, Wh, bh, out):
         block_codes = keep.tile([P, GATES, 2 * PACK, HALF], U32, name="block_codes", align_bytes=64)
         block_scales = keep.tile([P, GATES, 2 * PACK, HALF], U8, name="block_scales", align_bytes=64)
 
-        def prepare_weights(g):
+        def regroup_weights(g):
             for s in range(2):
                 nc.vector.tensor_copy(
                     out=w_grouped[:, g, s],
                     in_=w_raw[:, g, s].rearrange("p j (m t) -> p t m j", t=PACK),
                 )
+
+        def quantise_weights(g):
             nc.vector.quantize_mx(
                 out=block_codes[:, g].rearrange("p a m -> p (a m)").bitcast(FP8X4),
                 scales=block_scales[:, g].rearrange("p a m -> p (a m)"),
                 in_=w_grouped[:, g].rearrange("p s t m j -> p (s t m j)"),
             )
-            for half in range(2):
-                rows = slice(half * HALF, (half + 1) * HALF)
-                cols = slice(half * HALF, (half + 1) * HALF)
+
+        def place_weights(g):
+            for part in halves():
                 nc.vector.tensor_copy(
-                    out=w_codes[rows, g, :, cols].bitcast(I32), in_=block_codes[rows, g].bitcast(I32)
+                    out=w_codes[part, g, :, part].bitcast(I32), in_=block_codes[part, g].bitcast(I32)
                 )
                 nc.vector.tensor_copy(
-                    out=w_scales[rows, g, :, cols].bitcast(I32), in_=block_scales[rows, g].bitcast(I32)
+                    out=w_scales[part, g, :, part].bitcast(I32), in_=block_scales[part, g].bitcast(I32)
                 )
 
         squares = keep.tile([P, 2, ROWS * D], BF16, name="squares")
         sumsq = keep.tile([P, 2, ROWS], F32, name="sumsq")
+        floored = keep.tile([P, 2, ROWS], F32, name="floored")
         norm = keep.tile([P, 2, ROWS], F32, name="norm")
         inv_norm = keep.tile([P, 2, ROWS], F32, name="inv_norm")
         ln_plus = keep.tile([P, 2, ROWS], F32, name="ln_plus")
@@ -134,15 +140,18 @@ def tile_hyperbolicgru_kernel(tc, x, h, Wr, br, Wz, bz, Wh, bh, out):
                         func=ACT.Square,
                         accum_out=sumsq[:, o, r : r + 1],
                     )
-                nc.gpsimd.tensor_tensor(out=norm[:, o, rows], in0=sumsq[:, o, rows], in1=one_half[:], op=ALU.pow)
+                nc.gpsimd.tensor_scalar_max(out=floored[:, o, rows], in0=sumsq[:, o, rows], scalar1=TINY)
+                nc.gpsimd.tensor_tensor(out=norm[:, o, rows], in0=floored[:, o, rows], in1=one_half[:], op=ALU.pow)
 
-        def factors(k):
+        def logarithms(k):
             rows = chunk_rows(k)
             nc.scalar.activation(out=ln_plus[:, :, rows], in_=norm[:, :, rows], func=ACT.Ln, bias=1.0, scale=1.0)
             nc.scalar.activation(out=ln_minus[:, :, rows], in_=norm[:, :, rows], func=ACT.Ln, bias=1.0, scale=-1.0)
-            nc.vector.tensor_scalar_max(out=inv_norm[:, :, rows], in0=norm[:, :, rows], scalar1=TINY)
-            nc.vector.reciprocal(out=inv_norm[:, :, rows], in_=inv_norm[:, :, rows])
+            nc.vector.reciprocal(out=inv_norm[:, :, rows], in_=norm[:, :, rows])
             nc.vector.tensor_tensor(out=ln_diff[:, :, rows], in0=ln_plus[:, :, rows], in1=ln_minus[:, :, rows], op=ALU.subtract)
+
+        def row_factors(k):
+            rows = chunk_rows(k)
             nc.vector.scalar_tensor_tensor(
                 out=factor[:, :, rows], in0=ln_diff[:, :, rows], scalar=0.5, in1=inv_norm[:, :, rows],
                 op0=ALU.mult, op1=ALU.mult,
@@ -153,7 +162,7 @@ def tile_hyperbolicgru_kernel(tc, x, h, Wr, br, Wz, bz, Wh, bh, out):
         x_words = x_sb[:].bitcast(F32).rearrange("c (g p u) -> c g u p", p=P, u=2)
         h_words = h_sb[:].bitcast(F32).rearrange("c (g p u) -> c g u p", p=P, u=2)
 
-        def spread(k):
+        def spread_factors(k):
             repeated = work.tile([P, 2, CHUNK_ROWS, HALF], F32, name="repeated")
             nc.vector.tensor_copy(
                 out=repeated[:],
@@ -167,11 +176,14 @@ def tile_hyperbolicgru_kernel(tc, x, h, Wr, br, Wz, bz, Wh, bh, out):
                         in_=repeated[:, o, 2 * a : 2 * a + 2, :].rearrange("c r q -> c (r q)"),
                         identity=ident[:],
                     )
+            tiles["factor_ps", k] = factor_ps
+
+        def collect_factors(k):
             factor_t = work.tile([P, 2, CHUNK_COLS], F32, name="factor_t")
-            nc.scalar.copy(out=factor_t[:], in_=factor_ps[:])
+            nc.scalar.copy(out=factor_t[:], in_=tiles["factor_ps", k][:])
             tiles["factor_t", k] = factor_t
 
-        def turn(k):
+        def turn_words(k):
             for name, words in (("x_ps", x_words), ("h_ps", h_words)):
                 words_ps = turn_psum.tile([P, 2, CHUNK_COLS], F32, name="words_ps", tag="turn")
                 for a in range(CHUNK_PAIRS):
@@ -183,24 +195,25 @@ def tile_hyperbolicgru_kernel(tc, x, h, Wr, br, Wz, bz, Wh, bh, out):
                         )
                 tiles[name, k] = words_ps
 
-        def logmap(k):
-            factor_t = tiles["factor_t", k]
+        def logmap_x(k):
             xh_grouped = work.tile([P, 2, CHUNK_COLS, PACK], BF16, name="xh_grouped", align_bytes=64)
+            nc.vector.tensor_tensor(
+                out=xh_grouped[:, 0].rearrange("p c (u e) -> p c u e", u=2),
+                in0=tiles["x_ps", k][:].bitcast(BF16).rearrange("p u (c e) -> p c u e", e=2),
+                in1=tiles["factor_t", k][:, 0, :].unsqueeze(2).unsqueeze(3).to_broadcast([P, CHUNK_COLS, 2, 2]),
+                op=ALU.mult,
+            )
+            tiles["xh_grouped", k] = xh_grouped
+
+        def logmap_h(k):
             h_tan = held.tile([P, PACK, CHUNK_COLS], F32, name="h_tan")
             nc.vector.tensor_tensor(
                 out=h_tan[:].rearrange("p (u e) c -> p u e c", u=2),
                 in0=tiles["h_ps", k][:].bitcast(BF16).rearrange("p u (c e) -> p u e c", e=2),
-                in1=factor_t[:, 1, :].unsqueeze(1).unsqueeze(2).to_broadcast([P, 2, 2, CHUNK_COLS]),
+                in1=tiles["factor_t", k][:, 1, :].unsqueeze(1).unsqueeze(2).to_broadcast([P, 2, 2, CHUNK_COLS]),
                 op=ALU.mult,
             )
-            nc.scalar.copy(out=xh_grouped[:, 1], in_=h_tan[:].rearrange("p t c -> p c t"))
-            nc.vector.tensor_tensor(
-                out=xh_grouped[:, 0].rearrange("p c (u e) -> p c u e", u=2),
-                in0=tiles["x_ps", k][:].bitcast(BF16).rearrange("p u (c e) -> p c u e", e=2),
-                in1=factor_t[:, 0, :].unsqueeze(2).unsqueeze(3).to_broadcast([P, CHUNK_COLS, 2, 2]),
-                op=ALU.mult,
-            )
-            tiles["xh_grouped", k] = xh_grouped
+            nc.scalar.copy(out=tiles["xh_grouped", k][:, 1], in_=h_tan[:].rearrange("p t c -> p c t"))
             tiles["h_tan", k] = h_tan
 
         def quantise_xh(k):
@@ -232,7 +245,7 @@ def tile_hyperbolicgru_kernel(tc, x, h, Wr, br, Wz, bz, Wh, bh, out):
                 for i in range(2):
                     t = 2 * t_pair + i
                     nc.scalar.activation(
-                        out=result[:, t, :], in_=acc[:, i, :], func=func, bias=bias_bf[:, g, t : t + 1], scale=1.0
+                        out=result[:, t, :], in_=acc[:, i, :], func=func, bias=bias[:, g, t : t + 1], scale=1.0
                     )
 
         def gate_r(k):
@@ -245,7 +258,7 @@ def tile_hyperbolicgru_kernel(tc, x, h, Wr, br, Wz, bz, Wh, bh, out):
             gate(Z, ACT.Sigmoid, (tiles["x_mx", k], tiles["h_mx", k]), z_t)
             tiles["z_t", k] = z_t
 
-        def reset(k):
+        def reset_h(k):
             rh_grouped = work.tile([P, CHUNK_COLS, PACK], BF16, name="rh_grouped", align_bytes=64)
             nc.vector.tensor_tensor(
                 out=rh_grouped[:],
@@ -253,12 +266,15 @@ def tile_hyperbolicgru_kernel(tc, x, h, Wr, br, Wz, bz, Wh, bh, out):
                 in1=tiles["h_tan", k][:].rearrange("p t c -> p c t"),
                 op=ALU.mult,
             )
+            tiles["rh_grouped", k] = rh_grouped
+
+        def quantise_rh(k):
             rh_codes = work.tile([P, CHUNK_COLS], U32, name="rh_codes", align_bytes=64)
             rh_scales = work.tile([P, CHUNK_COLS], U8, name="rh_scales", align_bytes=64)
             nc.vector.quantize_mx(
                 out=rh_codes[:].bitcast(FP8X4),
                 scales=rh_scales[:],
-                in_=rh_grouped[:].rearrange("p c t -> p (c t)"),
+                in_=tiles["rh_grouped", k][:].rearrange("p c t -> p (c t)"),
             )
             tiles["rh_mx", k] = (rh_codes[:], rh_scales[:])
 
@@ -267,38 +283,41 @@ def tile_hyperbolicgru_kernel(tc, x, h, Wr, br, Wz, bz, Wh, bh, out):
             gate(N, ACT.Tanh, (tiles["x_mx", k], tiles["rh_mx", k]), n_t)
             tiles["n_t", k] = n_t
 
-        def mix(k):
+        def differ(k):
             n_t = tiles["n_t", k]
-            z_t = tiles["z_t", k]
             nc.vector.tensor_tensor(out=n_t[:], in0=n_t[:], in1=tiles["h_tan", k][:], op=ALU.subtract)
-            nc.vector.tensor_tensor(out=z_t[:], in0=z_t[:], in1=n_t[:], op=ALU.mult)
-            tiles["move_t", k] = z_t
+
+        def weigh(k):
+            z_t = tiles["z_t", k]
+            nc.vector.tensor_tensor(out=z_t[:], in0=z_t[:], in1=tiles["n_t", k][:], op=ALU.mult)
 
         def turn_back(k):
             for a in range(CHUNK_PAIRS):
                 move_ps = turn_psum.tile([P, PACK, P], F32, name="move_ps", tag="turn")
                 for t in range(PACK):
                     nc.tensor.transpose(
-                        out=move_ps[:, t, :], in_=tiles["move_t", k][:, t, a * P : (a + 1) * P], identity=ident[:]
+                        out=move_ps[:, t, :], in_=tiles["z_t", k][:, t, a * P : (a + 1) * P], identity=ident[:]
                     )
                 tiles["move_ps", k, a] = move_ps
 
         v_sumsq = keep.tile([P, ROWS], F32, name="v_sumsq")
+        v_floored = keep.tile([P, ROWS], F32, name="v_floored")
         v_norm = keep.tile([P, ROWS], F32, name="v_norm")
         v_inv = keep.tile([P, ROWS], F32, name="v_inv")
         v_tanh = keep.tile([P, ROWS], F32, name="v_tanh")
         v_factor = keep.tile([P, ROWS], F32, name="v_factor")
 
         def new_tangent(k):
+            rows = chunk_rows(k)
             v = held.tile([P, CHUNK_ROWS, D], F32, name="v")
             for i in range(CHUNK_ROWS):
                 r = k * CHUNK_ROWS + i
-                half = i % 2
+                part = halves()[i % 2]
                 nc.vector.scalar_tensor_tensor(
                     out=v[:, i, :].rearrange("c (q t) -> c q t", t=PACK),
                     in0=h_sb[:, r * D : (r + 1) * D].rearrange("c (q t) -> c q t", t=PACK),
                     scalar=factor[:, 1, r : r + 1],
-                    in1=tiles["move_ps", k, i // 2][:, :, half * HALF : (half + 1) * HALF].rearrange("c t q -> c q t"),
+                    in1=tiles["move_ps", k, i // 2][:, :, part].rearrange("c t q -> c q t"),
                     op0=ALU.mult,
                     op1=ALU.add,
                 )
@@ -306,20 +325,23 @@ def tile_hyperbolicgru_kernel(tc, x, h, Wr, br, Wz, bz, Wh, bh, out):
                     out=squares[:, 0, r * D : (r + 1) * D], in_=v[:, i, :], func=ACT.Square,
                     accum_out=v_sumsq[:, r : r + 1],
                 )
-            nc.gpsimd.tensor_tensor(out=v_norm[:, chunk_rows(k)], in0=v_sumsq[:, chunk_rows(k)], in1=one_half[:], op=ALU.pow)
+            nc.gpsimd.tensor_scalar_max(out=v_floored[:, rows], in0=v_sumsq[:, rows], scalar1=TINY)
+            nc.gpsimd.tensor_tensor(out=v_norm[:, rows], in0=v_floored[:, rows], in1=one_half[:], op=ALU.pow)
             tiles["v", k] = v
 
-        def tanh_of_norm(k):
-            nc.scalar.activation(out=v_tanh[:, chunk_rows(k)], in_=v_norm[:, chunk_rows(k)], func=ACT.Tanh)
-
-        def finish(k):
+        def radius(k):
             rows = chunk_rows(k)
-            nc.vector.tensor_scalar_max(out=v_inv[:, rows], in0=v_norm[:, rows], scalar1=TINY)
-            nc.vector.reciprocal(out=v_inv[:, rows], in_=v_inv[:, rows])
+            nc.scalar.activation(out=v_tanh[:, rows], in_=v_norm[:, rows], func=ACT.Tanh)
+            nc.vector.reciprocal(out=v_inv[:, rows], in_=v_norm[:, rows])
+
+        def shrink(k):
+            rows = chunk_rows(k)
             nc.vector.scalar_tensor_tensor(
                 out=v_factor[:, rows], in0=v_tanh[:, rows], scalar=MAX_NORM, in1=v_inv[:, rows],
                 op0=ALU.min, op1=ALU.mult,
             )
+
+        def finish(k):
             v = tiles["v", k]
             for a in range(CHUNK_PAIRS):
                 r = k * CHUNK_ROWS + 2 * a
@@ -338,25 +360,32 @@ def tile_hyperbolicgru_kernel(tc, x, h, Wr, br, Wz, bz, Wh, bh, out):
             if 0 <= k < count:
                 stage(k)
 
-        for j in range(-5, CHUNKS + 1):
-            staged(logmap, j)
-            staged(gate_r, j - 1)
-            staged(factors, j + 3)
+        for j in range(-5, CHUNKS + 3):
+            staged(spread_factors, j + 2)
+            staged(logmap_x, j)
+            staged(gate_r, j - 3)
+            staged(logarithms, j + 3)
+            staged(quantise_weights, j + 4, GATES)
+            staged(turn_words, j + 1)
             staged(norms, j + 5)
-            staged(turn, j + 1)
-            staged(spread, j + 2)
-            staged(prepare_weights, j + 4, GATES)
-            staged(quantise_xh, j)
+            staged(regroup_weights, j + 5, GATES)
+            staged(logmap_h, j)
+            staged(row_factors, j + 3)
+            staged(collect_factors, j + 2)
+            staged(quantise_xh, j - 1)
+            staged(place_weights, j + 4, GATES)
 
-        reset(0)
-        for k in range(CHUNKS):
-            gate_n(k)
-            gate_z(k)
-            staged(reset, k + 1)
+        for k in range(-2, CHUNKS + 1):
+            staged(reset_h, k + 2)
+            staged(quantise_rh, k + 1)
+            staged(gate_n, k)
+            staged(gate_z, k - 1)
 
-        for k in range(CHUNKS + 5):
-            staged(mix, k)
-            staged(new_tangent, k - 2)
-            staged(tanh_of_norm, k - 4)
-            staged(turn_back, k)
-            staged(finish, k - 5)
+        for k in range(CHUNKS + 6):
+            staged(differ, k)
+            staged(new_tangent, k - 3)
+            staged(shrink, k - 5)
+            staged(weigh, k - 1)
+            staged(finish, k - 6)
+            staged(radius, k - 4)
+            staged(turn_back, k - 2)

@@ -51,7 +51,7 @@ def tile_hyperbolicgru_kernel(tc, x, h, Wr, br, Wz, bz, Wh, bh, out):
         out_rows = out.rearrange("(c r) f -> c (r f)", r=ROWS)
         x_sb = keep.tile([P, ROWS * D], BF16, name="x_sb")
         h_sb = keep.tile([P, ROWS * D], BF16, name="h_sb")
-        w_raw = keep.tile([P, GATES, 2, PACK, D], BF16, name="w_raw")
+        w_raw = keep.tile([P, GATES, PACK, D], BF16, name="w_raw")
         bias = keep.tile([P, GATES, 16], BF16, name="bias")
 
         def load_rows(k):
@@ -60,9 +60,7 @@ def tile_hyperbolicgru_kernel(tc, x, h, Wr, br, Wz, bz, Wh, bh, out):
             nc.sync.dma_start(out=h_sb[:, cols], in_=h_rows[:, cols])
 
         def load_weights(g, w):
-            w_view = w.rearrange("(s q j) n -> q s j n", s=2, j=PACK)
-            for rows in halves():
-                nc.sync.dma_start(out=w_raw[rows, g], in_=w_view)
+            nc.sync.dma_start(out=w_raw[:, g], in_=w.rearrange("(p j) n -> p j n", j=PACK))
 
         def load_bias(g, b):
             b_view = b.rearrange("(q t) -> q t", t=PACK)
@@ -93,32 +91,32 @@ def tile_hyperbolicgru_kernel(tc, x, h, Wr, br, Wz, bz, Wh, bh, out):
         w_scales = keep.tile([P, GATES, 2 * PACK, P], U8, name="w_scales", align_bytes=64)
         nc.vector.memset(w_codes[:].bitcast(I32), 0)
         nc.vector.memset(w_scales[:].bitcast(I32), 0)
-        w_grouped = keep.tile([P, GATES, 2, PACK, HALF, PACK], BF16, name="w_grouped", align_bytes=64)
-        block_codes = keep.tile([P, GATES, 2 * PACK, HALF], U32, name="block_codes", align_bytes=64)
-        block_scales = keep.tile([P, GATES, 2 * PACK, HALF], U8, name="block_scales", align_bytes=64)
+        w_grouped = keep.tile([P, GATES, PACK, HALF, PACK], BF16, name="w_grouped", align_bytes=64)
+        block_codes = keep.tile([P, GATES, PACK, HALF], U32, name="block_codes", align_bytes=64)
+        block_scales = keep.tile([P, GATES, PACK, HALF], U8, name="block_scales", align_bytes=64)
 
         def regroup_weights(g):
-            for s in range(2):
-                nc.vector.tensor_copy(
-                    out=w_grouped[:, g, s],
-                    in_=w_raw[:, g, s].rearrange("p j (m t) -> p t m j", t=PACK),
-                )
+            nc.vector.tensor_copy(out=w_grouped[:, g], in_=w_raw[:, g].rearrange("p j (m t) -> p t m j", t=PACK))
 
         def quantise_weights(g):
             nc.vector.quantize_mx(
-                out=block_codes[:, g].rearrange("p a m -> p (a m)").bitcast(FP8X4),
-                scales=block_scales[:, g].rearrange("p a m -> p (a m)"),
-                in_=w_grouped[:, g].rearrange("p s t m j -> p (s t m j)"),
+                out=block_codes[:, g].rearrange("p t m -> p (t m)").bitcast(FP8X4),
+                scales=block_scales[:, g].rearrange("p t m -> p (t m)"),
+                in_=w_grouped[:, g].rearrange("p t m j -> p (t m j)"),
             )
 
         def place_weights(g):
-            for part in halves():
-                nc.vector.tensor_copy(
-                    out=w_codes[part, g, :, part].bitcast(I32), in_=block_codes[part, g].bitcast(I32)
-                )
-                nc.vector.tensor_copy(
-                    out=w_scales[part, g, :, part].bitcast(I32), in_=block_scales[part, g].bitcast(I32)
-                )
+            lower, upper = halves()
+            for s, own, other in ((0, lower, upper), (1, upper, lower)):
+                tiles_of_s = slice(s * PACK, (s + 1) * PACK)
+                for placed, block in ((w_codes, block_codes), (w_scales, block_scales)):
+                    nc.vector.tensor_copy(
+                        out=placed[own, g, tiles_of_s, own].bitcast(I32), in_=block[own, g].bitcast(I32)
+                    )
+                    with nc.allow_non_contiguous_dma(reason="a quarter of a tile: runs of 64 columns"):
+                        nc.sync.dma_start(
+                            out=placed[other, g, tiles_of_s, other].bitcast(I32), in_=block[own, g].bitcast(I32)
+                        )
 
         squares = keep.tile([P, 2, ROWS * D], BF16, name="squares")
         sumsq = keep.tile([P, 2, ROWS], F32, name="sumsq")

@@ -20,12 +20,14 @@ D = 256
 ROWS = BATCH // P
 CHUNKS = 4
 CHUNK_ROWS = ROWS // CHUNKS
-CHUNK_PAIRS = CHUNK_ROWS // 2
-CHUNK_COLS = CHUNK_PAIRS * P
+PAIRS = CHUNK_ROWS // 2
+COLS = PAIRS * P
 GATES = 3
 R, Z, N = 0, 1, 2
-TINY = 1e-30
+SLOTS = 2 * PACK + 1
+TINY = 1e-15
 MAX_NORM = 1.0 - 1e-5
+V_ROWS = 2
 
 FLOPS = 3 * 2 * BATCH * (2 * D) * D
 
@@ -43,8 +45,7 @@ def tile_hyperbolicgru_kernel(tc, x, h, Wr, br, Wz, bz, Wh, bh, out):
         def chunk_rows(k):
             return slice(k * CHUNK_ROWS, (k + 1) * CHUNK_ROWS)
 
-        def halves():
-            return (slice(0, HALF), slice(HALF, P))
+        halves = (slice(0, HALF), slice(HALF, P))
 
         x_rows = x.rearrange("(c r) f -> c (r f)", r=ROWS)
         h_rows = h.rearrange("(c r) f -> c (r f)", r=ROWS)
@@ -64,239 +65,286 @@ def tile_hyperbolicgru_kernel(tc, x, h, Wr, br, Wz, bz, Wh, bh, out):
 
         def load_bias(g, b):
             b_view = b.rearrange("(q t) -> q t", t=PACK)
-            for rows in halves():
+            for rows in halves:
                 nc.sync.dma_start(out=bias[rows, g, 0:PACK], in_=b_view)
 
         load_rows(0)
         load_weights(R, Wr)
         load_rows(1)
-        load_weights(Z, Wz)
-        load_rows(2)
         load_weights(N, Wh)
+        load_rows(2)
+        load_weights(Z, Wz)
         load_rows(3)
         with nc.allow_non_contiguous_dma(reason="four bias values to a partition"):
             load_bias(R, br)
             load_bias(Z, bz)
             load_bias(N, bh)
 
+        half_pow = keep.tile([P, 2, CHUNK_ROWS], F32, name="half_pow")
+        nc.gpsimd.memset(half_pow[:], 0.5)
         ident = keep.tile([P, P], F32, name="ident")
         make_identity(nc, ident[:])
-        one_half = keep.tile([P, CHUNK_ROWS], F32, name="one_half")
-        nc.gpsimd.memset(one_half[:], 0.5)
         warm = keep.tile([P, 2], F32, name="warm")
         nc.vector.memset(warm[:, 0:1], 1.0)
         nc.scalar.activation(out=warm[:, 1:2], in_=warm[:, 0:1], func=ACT.Ln)
 
-        w_codes = keep.tile([P, GATES, 2 * PACK, P], U32, name="w_codes", align_bytes=64)
-        w_scales = keep.tile([P, GATES, 2 * PACK, P], U8, name="w_scales", align_bytes=64)
-        nc.vector.memset(w_codes[:].bitcast(I32), 0)
-        nc.vector.memset(w_scales[:].bitcast(I32), 0)
+        w_codes = keep.tile([P, GATES, SLOTS * HALF], U32, name="w_codes", align_bytes=64)
+        w_scales = keep.tile([P, GATES, SLOTS * HALF], U8, name="w_scales", align_bytes=64)
+        bd_codes = keep.tile([P, PACK, P], U32, name="bd_codes", align_bytes=64)
+        bd_scales = keep.tile([P, PACK, P], U8, name="bd_scales", align_bytes=64)
+        nh_codes = keep.tile([P, PACK, HALF], U32, name="nh_codes", align_bytes=64)
+        nh_scales = keep.tile([P, PACK, HALF], U8, name="nh_scales", align_bytes=64)
         w_grouped = keep.tile([P, GATES, PACK, HALF, PACK], BF16, name="w_grouped", align_bytes=64)
-        block_codes = keep.tile([P, GATES, PACK, HALF], U32, name="block_codes", align_bytes=64)
-        block_scales = keep.tile([P, GATES, PACK, HALF], U8, name="block_scales", align_bytes=64)
+        minus_bias = keep.tile([P, PACK], F32, name="minus_bias")
 
-        def regroup_weights(g):
-            nc.vector.tensor_copy(out=w_grouped[:, g], in_=w_raw[:, g].rearrange("p j (m t) -> p t m j", t=PACK))
+        def slot_view(tile, g):
+            return tile[:, g].rearrange("p (b c) -> p b c", c=HALF)
+
+        for g in (R, Z):
+            nc.vector.memset(slot_view(w_codes, g)[:, 0:SLOTS:2, :].bitcast(I32), 0)
+            nc.vector.memset(slot_view(w_scales, g)[:, 0:SLOTS:2, :].bitcast(I32), 0)
+
+        nc.vector.memset(w_codes[:, N].bitcast(I32), 0)
+        nc.vector.memset(w_scales[:, N].bitcast(I32), 0)
+        nc.vector.memset(bd_codes[:].bitcast(I32), 0)
+        nc.vector.memset(bd_scales[:].bitcast(I32), 0)
+
+        def regroup_weights(g, copy):
+            copy(out=w_grouped[:, g], in_=w_raw[:, g].rearrange("p j (m t) -> p t m j", t=PACK))
 
         def quantise_weights(g):
+            for t in range(PACK):
+                at = slice((2 * t + 1) * HALF, (2 * t + 2) * HALF)
+                nc.vector.quantize_mx(
+                    out=w_codes[:, g, at].bitcast(FP8X4),
+                    scales=w_scales[:, g, at],
+                    in_=w_grouped[:, g, t].rearrange("p m j -> p (m j)"),
+                )
+
+        def quantise_n():
             nc.vector.quantize_mx(
-                out=block_codes[:, g].rearrange("p t m -> p (t m)").bitcast(FP8X4),
-                scales=block_scales[:, g].rearrange("p t m -> p (t m)"),
-                in_=w_grouped[:, g].rearrange("p t m j -> p (t m j)"),
+                out=nh_codes[:].rearrange("p t m -> p (t m)").bitcast(FP8X4),
+                scales=nh_scales[:].rearrange("p t m -> p (t m)"),
+                in_=w_grouped[:, N].rearrange("p t m j -> p (t m j)"),
             )
 
-        def place_weights(g):
-            lower, upper = halves()
-            for s, own, other in ((0, lower, upper), (1, upper, lower)):
-                tiles_of_s = slice(s * PACK, (s + 1) * PACK)
-                for placed, block in ((w_codes, block_codes), (w_scales, block_scales)):
-                    nc.vector.tensor_copy(
-                        out=placed[own, g, tiles_of_s, own].bitcast(I32), in_=block[own, g].bitcast(I32)
-                    )
-                    with nc.allow_non_contiguous_dma(reason="a quarter of a tile: runs of 64 columns"):
-                        nc.sync.dma_start(
-                            out=placed[other, g, tiles_of_s, other].bitcast(I32), in_=block[own, g].bitcast(I32)
-                        )
+        def place_n():
+            lower, upper = halves
+            for slots, diag, block in ((w_codes, bd_codes, nh_codes), (w_scales, bd_scales, nh_scales)):
+                nc.vector.tensor_copy(
+                    out=slot_view(slots, N)[lower, 1:SLOTS:2, :].bitcast(I32), in_=block[lower].bitcast(I32)
+                )
+                nc.vector.tensor_copy(out=diag[upper, :, upper].bitcast(I32), in_=block[upper].bitcast(I32))
+                with nc.allow_non_contiguous_dma(reason="a quarter of a tile: runs of 64 columns"):
+                    nc.sync.dma_start(out=diag[lower, :, lower].bitcast(I32), in_=block[upper].bitcast(I32))
 
         squares = keep.tile([P, 2, ROWS * D], BF16, name="squares")
         sumsq = keep.tile([P, 2, ROWS], F32, name="sumsq")
-        floored = keep.tile([P, 2, ROWS], F32, name="floored")
         norm = keep.tile([P, 2, ROWS], F32, name="norm")
-        inv_norm = keep.tile([P, 2, ROWS], F32, name="inv_norm")
+        twice = keep.tile([P, 2, ROWS], F32, name="twice")
+        inv_twice = keep.tile([P, 2, ROWS], F32, name="inv_twice")
         ln_plus = keep.tile([P, 2, ROWS], F32, name="ln_plus")
         ln_minus = keep.tile([P, 2, ROWS], F32, name="ln_minus")
         ln_diff = keep.tile([P, 2, ROWS], F32, name="ln_diff")
-        factor = keep.tile([P, 2, ROWS], F32, name="factor")
+
+        def sums_of_squares(k, o):
+            src = (x_sb, h_sb)[o]
+            for i in range(CHUNK_ROWS):
+                r = k * CHUNK_ROWS + i
+                cols = slice(r * D, (r + 1) * D)
+                if o == 1 and i < V_ROWS:
+                    nc.vector.scalar_tensor_tensor(
+                        out=squares[:, o, cols], in0=src[:, cols], scalar=1.0, in1=src[:, cols],
+                        op0=ALU.mult, op1=ALU.mult, accum_out=sumsq[:, o, r : r + 1],
+                    )
+                else:
+                    nc.scalar.activation(
+                        out=squares[:, o, cols], in_=src[:, cols], func=ACT.Square,
+                        accum_out=sumsq[:, o, r : r + 1],
+                    )
 
         def norms(k):
             rows = chunk_rows(k)
-            for o, src in enumerate((x_sb, h_sb)):
-                for r in range(k * CHUNK_ROWS, (k + 1) * CHUNK_ROWS):
-                    nc.scalar.activation(
-                        out=squares[:, o, r * D : (r + 1) * D],
-                        in_=src[:, r * D : (r + 1) * D],
-                        func=ACT.Square,
-                        accum_out=sumsq[:, o, r : r + 1],
-                    )
-                nc.gpsimd.tensor_scalar_max(out=floored[:, o, rows], in0=sumsq[:, o, rows], scalar1=TINY)
-                nc.gpsimd.tensor_tensor(out=norm[:, o, rows], in0=floored[:, o, rows], in1=one_half[:], op=ALU.pow)
+            nc.gpsimd.tensor_tensor(out=norm[:, :, rows], in0=sumsq[:, :, rows], in1=half_pow[:], op=ALU.pow)
 
         def logarithms(k):
             rows = chunk_rows(k)
             nc.scalar.activation(out=ln_plus[:, :, rows], in_=norm[:, :, rows], func=ACT.Ln, bias=1.0, scale=1.0)
             nc.scalar.activation(out=ln_minus[:, :, rows], in_=norm[:, :, rows], func=ACT.Ln, bias=1.0, scale=-1.0)
-            nc.vector.reciprocal(out=inv_norm[:, :, rows], in_=norm[:, :, rows])
-            nc.vector.tensor_tensor(out=ln_diff[:, :, rows], in0=ln_plus[:, :, rows], in1=ln_minus[:, :, rows], op=ALU.subtract)
 
-        def row_factors(k):
+        def inverses(k):
             rows = chunk_rows(k)
-            nc.vector.scalar_tensor_tensor(
-                out=factor[:, :, rows], in0=ln_diff[:, :, rows], scalar=0.5, in1=inv_norm[:, :, rows],
-                op0=ALU.mult, op1=ALU.mult,
+            nc.vector.tensor_scalar(
+                out=twice[:, :, rows], in0=norm[:, :, rows], scalar1=TINY, scalar2=2.0, op0=ALU.max, op1=ALU.mult
+            )
+            nc.vector.reciprocal(out=inv_twice[:, :, rows], in_=twice[:, :, rows])
+
+        def log_ratio(k):
+            rows = chunk_rows(k)
+            nc.vector.tensor_tensor(
+                out=ln_diff[:, :, rows], in0=ln_plus[:, :, rows], in1=ln_minus[:, :, rows], op=ALU.subtract
             )
 
         tiles = {}
 
-        x_words = x_sb[:].bitcast(F32).rearrange("c (g p u) -> c g u p", p=P, u=2)
-        h_words = h_sb[:].bitcast(F32).rearrange("c (g p u) -> c g u p", p=P, u=2)
-
-        def spread_factors(k):
-            repeated = work.tile([P, 2, CHUNK_ROWS, HALF], F32, name="repeated")
-            nc.vector.tensor_copy(
-                out=repeated[:],
-                in_=factor[:, :, chunk_rows(k)].unsqueeze(3).to_broadcast([P, 2, CHUNK_ROWS, HALF]),
-            )
-            factor_ps = turn_psum.tile([P, 2, CHUNK_COLS], F32, name="factor_ps", tag="turn")
-            for o in range(2):
-                for a in range(CHUNK_PAIRS):
-                    nc.tensor.transpose(
-                        out=factor_ps[:, o, a * P : (a + 1) * P],
-                        in_=repeated[:, o, 2 * a : 2 * a + 2, :].rearrange("c r q -> c (r q)"),
-                        identity=ident[:],
+        def tangents(k):
+            xh_tan = work.tile([P, CHUNK_ROWS, 2, 2, HALF, 2], BF16, name="xh_tan")
+            for i in range(CHUNK_ROWS):
+                r = k * CHUNK_ROWS + i
+                for o, src in enumerate((x_sb, h_sb)):
+                    nc.vector.tensor_scalar(
+                        out=xh_tan[:, i, :, o],
+                        in0=src[:, r * D : (r + 1) * D].rearrange("c (p u e) -> c u p e", u=2, e=2),
+                        scalar1=ln_diff[:, o, r : r + 1], scalar2=inv_twice[:, o, r : r + 1],
+                        op0=ALU.mult, op1=ALU.mult,
                     )
-            tiles["factor_ps", k] = factor_ps
+            tiles["xh_tan", k] = xh_tan
 
-        def collect_factors(k):
-            factor_t = work.tile([P, 2, CHUNK_COLS], F32, name="factor_t")
-            nc.scalar.copy(out=factor_t[:], in_=tiles["factor_ps", k][:])
-            tiles["factor_t", k] = factor_t
-
-        def turn_words(k):
-            for name, words in (("x_ps", x_words), ("h_ps", h_words)):
-                words_ps = turn_psum.tile([P, 2, CHUNK_COLS], F32, name="words_ps", tag="turn")
-                for a in range(CHUNK_PAIRS):
-                    for u in range(2):
-                        nc.tensor.transpose(
-                            out=words_ps[:, u, a * P : (a + 1) * P],
-                            in_=words[:, k * CHUNK_PAIRS + a, u, :],
-                            identity=ident[:],
-                        )
-                tiles[name, k] = words_ps
-
-        def logmap_x(k):
-            xh_grouped = work.tile([P, 2, CHUNK_COLS, PACK], BF16, name="xh_grouped", align_bytes=64)
-            nc.vector.tensor_tensor(
-                out=xh_grouped[:, 0].rearrange("p c (u e) -> p c u e", u=2),
-                in0=tiles["x_ps", k][:].bitcast(BF16).rearrange("p u (c e) -> p c u e", e=2),
-                in1=tiles["factor_t", k][:, 0, :].unsqueeze(2).unsqueeze(3).to_broadcast([P, CHUNK_COLS, 2, 2]),
-                op=ALU.mult,
-            )
-            tiles["xh_grouped", k] = xh_grouped
-
-        def logmap_h(k):
-            h_tan = held.tile([P, PACK, CHUNK_COLS], F32, name="h_tan")
-            nc.vector.tensor_tensor(
-                out=h_tan[:].rearrange("p (u e) c -> p u e c", u=2),
-                in0=tiles["h_ps", k][:].bitcast(BF16).rearrange("p u (c e) -> p u e c", e=2),
-                in1=tiles["factor_t", k][:, 1, :].unsqueeze(1).unsqueeze(2).to_broadcast([P, 2, 2, CHUNK_COLS]),
-                op=ALU.mult,
-            )
-            nc.scalar.copy(out=tiles["xh_grouped", k][:, 1], in_=h_tan[:].rearrange("p t c -> p c t"))
+        def h_tangent(k):
+            h_tan = held.tile([P, PAIRS, PACK, 2, HALF], F32, name="h_tan")
+            for i in range(CHUNK_ROWS):
+                r = k * CHUNK_ROWS + i
+                nc.gpsimd.tensor_scalar(
+                    out=h_tan[:, i // 2, :, i % 2, :],
+                    in0=h_sb[:, r * D : (r + 1) * D].rearrange("c (q t) -> c t q", t=PACK),
+                    scalar1=ln_diff[:, 1, r : r + 1], scalar2=inv_twice[:, 1, r : r + 1],
+                    op0=ALU.mult, op1=ALU.mult,
+                )
             tiles["h_tan", k] = h_tan
 
-        def quantise_xh(k):
-            xh_codes = held.tile([P, 2, CHUNK_COLS], U32, name="xh_codes", align_bytes=64)
-            xh_scales = held.tile([P, 2, CHUNK_COLS], U8, name="xh_scales", align_bytes=64)
-            nc.vector.quantize_mx(
-                out=xh_codes[:].rearrange("p o c -> p (o c)").bitcast(FP8X4),
-                scales=xh_scales[:].rearrange("p o c -> p (o c)"),
-                in_=tiles["xh_grouped", k][:].rearrange("p o c t -> p (o c t)"),
-            )
-            tiles["x_mx", k] = (xh_codes[:, 0, :], xh_scales[:, 0, :])
-            tiles["h_mx", k] = (xh_codes[:, 1, :], xh_scales[:, 1, :])
-
-        def gate(g, func, operands, result):
-            for t_pair in range(2):
-                acc = gate_psum.tile([P, 2, CHUNK_COLS], F32, name="acc")
-                for i in range(2):
-                    t = 2 * t_pair + i
-                    for s, (codes, scales) in enumerate(operands):
-                        nc.tensor.matmul_mx(
-                            out=acc[:, i, :],
-                            lhsT=w_codes[:, g, s * PACK + t, :].bitcast(FP8X4),
-                            lhsT_scale=w_scales[:, g, s * PACK + t, :],
-                            rhs=codes.bitcast(FP8X4),
-                            rhs_scale=scales,
-                            start=(s == 0),
-                            stop=(s == 1),
+        def turn_words(k):
+            words = tiles["xh_tan", k][:].rearrange("c i u o p e -> c (i u o p e)").bitcast(F32)
+            for s in range(2):
+                words_ps = turn_psum.tile([P, 2, COLS], F32, name="words_ps", tag="turn")
+                for a in range(PAIRS):
+                    for u in range(2):
+                        at = ((2 * a + s) * 2 + u) * P
+                        nc.tensor.transpose(
+                            out=words_ps[:, u, a * P : (a + 1) * P], in_=words[:, at : at + P], identity=ident[:]
                         )
+                tiles["words_ps", k, s] = words_ps
+
+        def collect_words(k, s, copy):
+            if s == 0:
+                tiles["grouped", k] = work.tile([P, 2, COLS, PACK], BF16, name="grouped", align_bytes=64)
+            copy(
+                out=tiles["grouped", k][:, s].rearrange("p c t -> p (c t)").bitcast(F32).rearrange("p (c u) -> p c u", u=2),
+                in_=tiles["words_ps", k, s][:].rearrange("p u c -> p c u"),
+            )
+
+        def collect_even(k):
+            collect_words(k, 0, nc.vector.tensor_copy)
+
+        def collect_odd(k):
+            collect_words(k, 1, nc.scalar.copy)
+
+        def quantise_xh(k):
+            xh_codes = held.tile([P, 2, COLS], U32, name="xh_codes", align_bytes=64)
+            xh_scales = held.tile([P, 2, COLS], U8, name="xh_scales", align_bytes=64)
+            nc.vector.quantize_mx(
+                out=xh_codes[:].rearrange("p s c -> p (s c)").bitcast(FP8X4),
+                scales=xh_scales[:].rearrange("p s c -> p (s c)"),
+                in_=tiles["grouped", k][:].rearrange("p s c t -> p (s c t)"),
+            )
+            tiles["xh_mx", k] = (xh_codes, xh_scales)
+
+        def xh_passes(g, t, k):
+            codes, scales = tiles["xh_mx", k]
+            passes = []
+            for s in range(2):
+                at = slice((2 * t + 1 - s) * HALF, (2 * t + 3 - s) * HALF)
+                passes.append((w_codes[:, g, at], w_scales[:, g, at], codes[:, s, :], scales[:, s, :]))
+            return passes
+
+        def rh_pass(t, k):
+            codes, scales = tiles["rh_mx", k]
+            return [(bd_codes[:, t], bd_scales[:, t], codes[:], scales[:])]
+
+        def gate(g, k):
+            for t_pair in range(2):
+                acc = gate_psum.tile([P, 2, COLS], F32, name="acc")
                 for i in range(2):
                     t = 2 * t_pair + i
-                    nc.scalar.activation(
-                        out=result[:, t, :], in_=acc[:, i, :], func=func, bias=bias[:, g, t : t + 1], scale=1.0
-                    )
+                    passes = xh_passes(g, t, k) + (rh_pass(t, k) if g == N else [])
+                    for n, (lhs, lhs_scale, rhs, rhs_scale) in enumerate(passes):
+                        nc.tensor.matmul_mx(
+                            out=acc[:, i, :], lhsT=lhs.bitcast(FP8X4), lhsT_scale=lhs_scale,
+                            rhs=rhs.bitcast(FP8X4), rhs_scale=rhs_scale,
+                            start=(n == 0), stop=(n == len(passes) - 1),
+                        )
+                tiles["acc", g, k, t_pair] = acc
 
-        def gate_r(k):
-            r_t = held.tile([P, PACK, CHUNK_COLS], F32, name="r_t")
-            gate(R, ACT.Sigmoid, (tiles["x_mx", k], tiles["h_mx", k]), r_t)
-            tiles["r_t", k] = r_t
+        def activate(g, k):
+            result = held.tile([P, PACK, COLS], F32, name="gate_" + "rzn"[g])
+            for t in range(PACK):
+                nc.scalar.activation(
+                    out=result[:, t, :], in_=tiles["acc", g, k, t // 2][:, t % 2, :],
+                    func=ACT.Tanh if g == N else ACT.Sigmoid,
+                    bias=minus_bias[:, t : t + 1] if g == N else bias[:, g, t : t + 1],
+                    scale=-1.0 if g == N else 1.0,
+                )
+            tiles["rzn"[g] + "_t", k] = result
 
-        def gate_z(k):
-            z_t = held.tile([P, PACK, CHUNK_COLS], F32, name="z_t")
-            gate(Z, ACT.Sigmoid, (tiles["x_mx", k], tiles["h_mx", k]), z_t)
-            tiles["z_t", k] = z_t
-
-        def reset_h(k):
-            rh_grouped = work.tile([P, CHUNK_COLS, PACK], BF16, name="rh_grouped", align_bytes=64)
-            nc.vector.tensor_tensor(
-                out=rh_grouped[:],
-                in0=tiles["r_t", k][:].rearrange("p t c -> p c t"),
-                in1=tiles["h_tan", k][:].rearrange("p t c -> p c t"),
-                op=ALU.mult,
-            )
-            tiles["rh_grouped", k] = rh_grouped
-
-        def quantise_rh(k):
-            rh_codes = work.tile([P, CHUNK_COLS], U32, name="rh_codes", align_bytes=64)
-            rh_scales = work.tile([P, CHUNK_COLS], U8, name="rh_scales", align_bytes=64)
-            nc.vector.quantize_mx(
-                out=rh_codes[:].bitcast(FP8X4),
-                scales=rh_scales[:],
-                in_=tiles["rh_grouped", k][:].rearrange("p c t -> p (c t)"),
-            )
-            tiles["rh_mx", k] = (rh_codes[:], rh_scales[:])
-
-        def gate_n(k):
-            n_t = held.tile([P, PACK, CHUNK_COLS], F32, name="n_t")
-            gate(N, ACT.Tanh, (tiles["x_mx", k], tiles["rh_mx", k]), n_t)
-            tiles["n_t", k] = n_t
-
-        def differ(k):
-            n_t = tiles["n_t", k]
-            nc.vector.tensor_tensor(out=n_t[:], in0=n_t[:], in1=tiles["h_tan", k][:], op=ALU.subtract)
-
-        def weigh(k):
-            z_t = tiles["z_t", k]
-            nc.vector.tensor_tensor(out=z_t[:], in0=z_t[:], in1=tiles["n_t", k][:], op=ALU.mult)
-
-        def turn_back(k):
-            for a in range(CHUNK_PAIRS):
-                move_ps = turn_psum.tile([P, PACK, P], F32, name="move_ps", tag="turn")
+        def turn_h(k):
+            for a in range(PAIRS):
+                h_ps = turn_psum.tile([P, PACK, P], F32, name="h_ps", tag="turn")
                 for t in range(PACK):
                     nc.tensor.transpose(
-                        out=move_ps[:, t, :], in_=tiles["z_t", k][:, t, a * P : (a + 1) * P], identity=ident[:]
+                        out=h_ps[:, t, :], in_=tiles["h_tan", k][:, a, t].rearrange("c r q -> c (r q)"),
+                        identity=ident[:],
                     )
-                tiles["move_ps", k, a] = move_ps
+                tiles["h_ps", k, a] = h_ps
+
+        def reset_h(k):
+            rh_grouped = work.tile([P, COLS, PACK], BF16, name="rh_grouped", align_bytes=64)
+            for a in range(PAIRS):
+                cols = slice(a * P, (a + 1) * P)
+                nc.vector.tensor_tensor(
+                    out=rh_grouped[:, cols, :],
+                    in0=tiles["h_ps", k, a][:].rearrange("p t c -> p c t"),
+                    in1=tiles["r_t", k][:, :, cols].rearrange("p t c -> p c t"),
+                    op=ALU.mult,
+                )
+            tiles["rh_grouped", k] = rh_grouped
+
+        def keep_h(k):
+            kept = held.tile([P, PACK, COLS], F32, name="kept")
+            for a in range(PAIRS):
+                cols = slice(a * P, (a + 1) * P)
+                nc.vector.scalar_tensor_tensor(
+                    out=kept[:, :, cols], in0=tiles["z_t", k][:, :, cols], scalar=1.0, in1=tiles["h_ps", k, a][:],
+                    op0=ALU.subtract, op1=ALU.mult,
+                )
+            tiles["kept", k] = kept
+
+        def quantise_rh(k):
+            rh_codes = work.tile([P, COLS], U32, name="rh_codes", align_bytes=64)
+            rh_scales = work.tile([P, COLS], U8, name="rh_scales", align_bytes=64)
+            nc.vector.quantize_mx(
+                out=rh_codes[:].bitcast(FP8X4), scales=rh_scales[:],
+                in_=tiles["rh_grouped", k][:].rearrange("p c t -> p (c t)"),
+            )
+            tiles["rh_mx", k] = (rh_codes, rh_scales)
+
+        def take_n(k):
+            taken = held.tile([P, PACK, COLS], F32, name="taken")
+            for engine, part in ((nc.gpsimd, slice(0, 2)), (nc.vector, slice(2, 4))):
+                engine.tensor_tensor(
+                    out=taken[:, part], in0=tiles["z_t", k][:, part], in1=tiles["n_t", k][:, part], op=ALU.mult
+                )
+            tiles["taken", k] = taken
+
+        def turn_back(k):
+            for a in range(PAIRS):
+                cols = slice(a * P, (a + 1) * P)
+                v_ps = turn_psum.tile([P, PACK, P], F32, name="v_ps", tag="turn")
+                for t in range(PACK):
+                    for n, part in enumerate(("kept", "taken")):
+                        nc.tensor.matmul(
+                            out=v_ps[:, t, :], lhsT=tiles[part, k][:, t, cols], rhs=ident[:],
+                            start=(n == 0), stop=(n == 1), is_transpose=True,
+                        )
+                tiles["v_ps", k, a] = v_ps
 
         v_sumsq = keep.tile([P, ROWS], F32, name="v_sumsq")
         v_floored = keep.tile([P, ROWS], F32, name="v_floored")
@@ -305,85 +353,128 @@ def tile_hyperbolicgru_kernel(tc, x, h, Wr, br, Wz, bz, Wh, bh, out):
         v_tanh = keep.tile([P, ROWS], F32, name="v_tanh")
         v_factor = keep.tile([P, ROWS], F32, name="v_factor")
 
-        def new_tangent(k):
+        def new_norms(k):
             rows = chunk_rows(k)
-            v = held.tile([P, CHUNK_ROWS, D], F32, name="v")
             for i in range(CHUNK_ROWS):
                 r = k * CHUNK_ROWS + i
-                part = halves()[i % 2]
-                nc.vector.scalar_tensor_tensor(
-                    out=v[:, i, :].rearrange("c (q t) -> c q t", t=PACK),
-                    in0=h_sb[:, r * D : (r + 1) * D].rearrange("c (q t) -> c q t", t=PACK),
-                    scalar=factor[:, 1, r : r + 1],
-                    in1=tiles["move_ps", k, i // 2][:, :, part].rearrange("c t q -> c q t"),
-                    op0=ALU.mult,
-                    op1=ALU.add,
-                )
                 nc.scalar.activation(
-                    out=squares[:, 0, r * D : (r + 1) * D], in_=v[:, i, :], func=ACT.Square,
+                    out=squares[:, 0, r * D : (r + 1) * D].rearrange("c (t q) -> c t q", t=PACK),
+                    in_=tiles["v_ps", k, i // 2][:, :, halves[i % 2]], func=ACT.Square,
                     accum_out=v_sumsq[:, r : r + 1],
                 )
-            nc.gpsimd.tensor_scalar_max(out=v_floored[:, rows], in0=v_sumsq[:, rows], scalar1=TINY)
-            nc.gpsimd.tensor_tensor(out=v_norm[:, rows], in0=v_floored[:, rows], in1=one_half[:], op=ALU.pow)
-            tiles["v", k] = v
+            nc.gpsimd.tensor_tensor(out=v_norm[:, rows], in0=v_sumsq[:, rows], in1=half_pow[:, 0], op=ALU.pow)
 
         def radius(k):
             rows = chunk_rows(k)
-            nc.scalar.activation(out=v_tanh[:, rows], in_=v_norm[:, rows], func=ACT.Tanh)
-            nc.vector.reciprocal(out=v_inv[:, rows], in_=v_norm[:, rows])
+            nc.scalar.activation(out=v_tanh[:, rows], in_=v_norm[:, rows], func=ACT.Tanh, scale=-1.0)
+            nc.vector.tensor_scalar_max(out=v_floored[:, rows], in0=v_norm[:, rows], scalar1=TINY)
+            nc.vector.reciprocal(out=v_inv[:, rows], in_=v_floored[:, rows])
 
         def shrink(k):
             rows = chunk_rows(k)
             nc.vector.scalar_tensor_tensor(
-                out=v_factor[:, rows], in0=v_tanh[:, rows], scalar=MAX_NORM, in1=v_inv[:, rows],
-                op0=ALU.min, op1=ALU.mult,
+                out=v_factor[:, rows], in0=v_tanh[:, rows], scalar=-MAX_NORM, in1=v_inv[:, rows],
+                op0=ALU.max, op1=ALU.mult,
             )
 
         def finish(k):
-            v = tiles["v", k]
-            for a in range(CHUNK_PAIRS):
+            out_sb = held.tile([P, CHUNK_ROWS, D], F32, name="out_sb")
+            for a in range(PAIRS):
                 r = k * CHUNK_ROWS + 2 * a
+                v_ps = tiles["v_ps", k, a]
                 nc.scalar.activation(
-                    out=v[:, 2 * a, :], in_=v[:, 2 * a, :], func=ACT.Copy, scale=v_factor[:, r : r + 1]
+                    out=out_sb[:, 2 * a, :].rearrange("c (q t) -> c q t", t=PACK),
+                    in_=v_ps[:, :, halves[0]].rearrange("c t q -> c q t"),
+                    func=ACT.Copy, scale=v_factor[:, r : r + 1],
                 )
                 nc.vector.tensor_scalar_mul(
-                    out=v[:, 2 * a + 1, :], in0=v[:, 2 * a + 1, :], scalar1=v_factor[:, r + 1 : r + 2]
+                    out=out_sb[:, 2 * a + 1, :].rearrange("c (q t) -> c q t", t=PACK),
+                    in0=v_ps[:, :, halves[1]].rearrange("c t q -> c q t"),
+                    scalar1=v_factor[:, r + 1 : r + 2],
                 )
                 nc.sync.dma_start(
                     out=out_rows[:, r * D : (r + 2) * D],
-                    in_=v[:, 2 * a : 2 * a + 2, :].rearrange("c r f -> c (r f)"),
+                    in_=out_sb[:, 2 * a : 2 * a + 2, :].rearrange("c r f -> c (r f)"),
                 )
 
-        def staged(stage, k, count=CHUNKS):
-            if 0 <= k < count:
-                stage(k)
+        def staged(stage, k, *args):
+            if 0 <= k < CHUNKS:
+                stage(k, *args)
 
-        for j in range(-5, CHUNKS + 3):
-            staged(spread_factors, j + 2)
-            staged(logmap_x, j)
-            staged(gate_r, j - 3)
-            staged(logarithms, j + 3)
-            staged(quantise_weights, j + 4, GATES)
-            staged(turn_words, j + 1)
-            staged(norms, j + 5)
-            staged(regroup_weights, j + 5, GATES)
-            staged(logmap_h, j)
-            staged(row_factors, j + 3)
-            staged(collect_factors, j + 2)
+        def sums(k):
+            sums_of_squares(k, 0)
+            sums_of_squares(k, 1)
+            norms(k)
+
+        sums(0)
+        regroup_weights(R, nc.vector.tensor_copy)
+        sums(1)
+        quantise_weights(R)
+        sums(2)
+        logarithms(0)
+        sums_of_squares(3, 0)
+        logarithms(1)
+        sums_of_squares(3, 1)
+        norms(3)
+        nc.vector.tensor_scalar_mul(out=minus_bias[:], in0=bias[:, N, 0:PACK], scalar1=-1.0)
+        for j in range(CHUNKS + 2):
+            staged(inverses, j)
+            staged(collect_even, j - 1)
+            if j == 1:
+                collect_odd(0)
+            if j >= 2:
+                staged(logarithms, j)
+            if j == 2:
+                regroup_weights(Z, nc.scalar.copy)
+            if j == 3:
+                activate(R, 0)
+            if j == 4:
+                activate(R, 1)
+                regroup_weights(N, nc.scalar.copy)
+            staged(log_ratio, j)
+            if j > 2:
+                staged(collect_odd, j - 1)
+            if j == 2:
+                collect_odd(1)
+            if j == 5:
+                activate(Z, 0)
+            if j == 3:
+                quantise_weights(Z)
+            if j == 4:
+                reset_h(0)
+                quantise_rh(0)
             staged(quantise_xh, j - 1)
-            staged(place_weights, j + 4, GATES)
-
-        for k in range(-2, CHUNKS + 1):
-            staged(reset_h, k + 2)
-            staged(quantise_rh, k + 1)
-            staged(gate_n, k)
-            staged(gate_z, k - 1)
-
-        for k in range(CHUNKS + 6):
-            staged(differ, k)
-            staged(new_tangent, k - 3)
-            staged(shrink, k - 5)
-            staged(weigh, k - 1)
-            staged(finish, k - 6)
-            staged(radius, k - 4)
-            staged(turn_back, k - 2)
+            staged(tangents, j)
+            if j in (1, 2):
+                gate(R, j - 1)
+            staged(turn_words, j)
+            staged(h_tangent, j)
+            if j == 3:
+                turn_h(0)
+                gate(Z, 0)
+            if j == 4:
+                turn_h(1)
+                quantise_n()
+                place_n()
+            if j == 5:
+                keep_h(0)
+        for i in range(1, CHUNKS + 4):
+            if i + 1 < CHUNKS:
+                gate(R, i + 1)
+                activate(R, i + 1)
+            if i < CHUNKS:
+                gate(Z, i)
+                activate(Z, i)
+            staged(reset_h, i)
+            staged(quantise_rh, i)
+            staged(keep_h, i)
+            staged(turn_h, i + 1)
+            if i <= CHUNKS:
+                gate(N, i - 1)
+                activate(N, i - 1)
+            staged(take_n, i - 1)
+            staged(turn_back, i - 2)
+            staged(new_norms, i - 2)
+            staged(radius, i - 3)
+            staged(shrink, i - 3)
+            staged(finish, i - 3)

@@ -112,6 +112,9 @@ def tile_hyperbolicgru_kernel(tc, x, h, Wr, br, Wz, bz, Wh, bh, out):
         def regroup_weights(g, copy):
             copy(out=w_grouped[:, g], in_=w_raw[:, g].rearrange("p j (m t) -> p t m j", t=PACK))
 
+        def gpsimd_copy(out, in_):
+            nc.gpsimd.tensor_scalar(out=out, in0=in_, scalar1=1.0, scalar2=0.0, op0=ALU.mult, op1=ALU.add)
+
         def quantise_weights(g):
             for t in range(PACK):
                 at = slice((2 * t + 1) * HALF, (2 * t + 2) * HALF)
@@ -308,18 +311,18 @@ def tile_hyperbolicgru_kernel(tc, x, h, Wr, br, Wz, bz, Wh, bh, out):
             tiles["rh_grouped", k] = rh_grouped
 
         def keep_h(k):
-            kept = held.tile([P, PACK, COLS], F32, name="kept")
             for a in range(PAIRS):
                 cols = slice(a * P, (a + 1) * P)
+                kept = held.tile([P, PACK, P], F32, name=f"kept_{a}")
                 nc.vector.scalar_tensor_tensor(
-                    out=kept[:, :, cols], in0=tiles["z_t", k][:, :, cols], scalar=1.0, in1=tiles["h_ps", k, a][:],
+                    out=kept[:], in0=tiles["z_t", k][:, :, cols], scalar=1.0, in1=tiles["h_ps", k, a][:],
                     op0=ALU.subtract, op1=ALU.mult,
                 )
-            tiles["kept", k] = kept
+                tiles["kept", k, a] = kept
 
         def quantise_rh(k):
-            rh_codes = work.tile([P, COLS], U32, name="rh_codes", align_bytes=64)
-            rh_scales = work.tile([P, COLS], U8, name="rh_scales", align_bytes=64)
+            rh_codes = held.tile([P, COLS], U32, name="rh_codes", align_bytes=64)
+            rh_scales = held.tile([P, COLS], U8, name="rh_scales", align_bytes=64)
             nc.vector.quantize_mx(
                 out=rh_codes[:].bitcast(FP8X4), scales=rh_scales[:],
                 in_=tiles["rh_grouped", k][:].rearrange("p c t -> p (c t)"),
@@ -327,74 +330,78 @@ def tile_hyperbolicgru_kernel(tc, x, h, Wr, br, Wz, bz, Wh, bh, out):
             tiles["rh_mx", k] = (rh_codes, rh_scales)
 
         def take_n(k):
-            taken = held.tile([P, PACK, COLS], F32, name="taken")
-            for engine, part in ((nc.gpsimd, slice(0, 2)), (nc.vector, slice(2, 4))):
-                engine.tensor_tensor(
-                    out=taken[:, part], in0=tiles["z_t", k][:, part], in1=tiles["n_t", k][:, part], op=ALU.mult
-                )
-            tiles["taken", k] = taken
-
-        def turn_back(k):
-            for a in range(PAIRS):
+            for a, engine in ((0, nc.vector), (1, nc.gpsimd)):
                 cols = slice(a * P, (a + 1) * P)
+                taken = held.tile([P, PACK, P], F32, name=f"taken_{a}")
+                engine.tensor_tensor(
+                    out=taken[:], in0=tiles["z_t", k][:, :, cols], in1=tiles["n_t", k][:, :, cols], op=ALU.mult
+                )
+                tiles["taken", k, a] = taken
+
+        def turn_back(k, a):
+            if k < CHUNKS // 2:
                 v_ps = turn_psum.tile([P, PACK, P], F32, name="v_ps", tag="turn")
-                for t in range(PACK):
-                    for n, part in enumerate(("kept", "taken")):
-                        nc.tensor.matmul(
-                            out=v_ps[:, t, :], lhsT=tiles[part, k][:, t, cols], rhs=ident[:],
-                            start=(n == 0), stop=(n == 1), is_transpose=True,
-                        )
-                tiles["v_ps", k, a] = v_ps
+            else:
+                v_ps = gate_psum.tile([P, PACK, P], F32, name="v_ps", tag="acc")
+            for t in range(PACK):
+                for n, part in enumerate(("kept", "taken")):
+                    nc.tensor.matmul(
+                        out=v_ps[:, t, :], lhsT=tiles[part, k, a][:, t, :], rhs=ident[:],
+                        start=(n == 0), stop=(n == 1), is_transpose=True,
+                    )
+            tiles["v_ps", k, a] = v_ps
 
         v_sumsq = keep.tile([P, ROWS], F32, name="v_sumsq")
-        v_floored = keep.tile([P, ROWS], F32, name="v_floored")
         v_norm = keep.tile([P, ROWS], F32, name="v_norm")
+        v_floored = keep.tile([P, ROWS], F32, name="v_floored")
         v_inv = keep.tile([P, ROWS], F32, name="v_inv")
         v_tanh = keep.tile([P, ROWS], F32, name="v_tanh")
         v_factor = keep.tile([P, ROWS], F32, name="v_factor")
 
-        def new_norms(k):
-            rows = chunk_rows(k)
-            for i in range(CHUNK_ROWS):
-                r = k * CHUNK_ROWS + i
-                nc.scalar.activation(
-                    out=squares[:, 0, r * D : (r + 1) * D].rearrange("c (t q) -> c t q", t=PACK),
-                    in_=tiles["v_ps", k, i // 2][:, :, halves[i % 2]], func=ACT.Square,
-                    accum_out=v_sumsq[:, r : r + 1],
-                )
-            nc.gpsimd.tensor_tensor(out=v_norm[:, rows], in0=v_sumsq[:, rows], in1=half_pow[:, 0], op=ALU.pow)
+        def pair_rows(k, pairs):
+            return slice(k * CHUNK_ROWS + 2 * pairs[0], k * CHUNK_ROWS + 2 * pairs[-1] + 2)
 
-        def radius(k):
-            rows = chunk_rows(k)
+        def new_norms(k, pairs):
+            for a in pairs:
+                for i in range(2):
+                    r = k * CHUNK_ROWS + 2 * a + i
+                    nc.scalar.activation(
+                        out=squares[:, 0, r * D : (r + 1) * D].rearrange("c (t q) -> c t q", t=PACK),
+                        in_=tiles["v_ps", k, a][:, :, halves[i]], func=ACT.Square,
+                        accum_out=v_sumsq[:, r : r + 1],
+                    )
+            rows = pair_rows(k, pairs)
+            nc.gpsimd.tensor_tensor(
+                out=v_norm[:, rows], in0=v_sumsq[:, rows], in1=half_pow[:, 0, 0 : 2 * len(pairs)], op=ALU.pow
+            )
+
+        def radius(k, pairs):
+            rows = pair_rows(k, pairs)
             nc.scalar.activation(out=v_tanh[:, rows], in_=v_norm[:, rows], func=ACT.Tanh, scale=-1.0)
             nc.vector.tensor_scalar_max(out=v_floored[:, rows], in0=v_norm[:, rows], scalar1=TINY)
             nc.vector.reciprocal(out=v_inv[:, rows], in_=v_floored[:, rows])
-
-        def shrink(k):
-            rows = chunk_rows(k)
             nc.vector.scalar_tensor_tensor(
                 out=v_factor[:, rows], in0=v_tanh[:, rows], scalar=-MAX_NORM, in1=v_inv[:, rows],
                 op0=ALU.max, op1=ALU.mult,
             )
 
-        def finish(k):
-            out_sb = held.tile([P, CHUNK_ROWS, D], F32, name="out_sb")
-            for a in range(PAIRS):
+        def finish(k, pairs):
+            for a in pairs:
                 r = k * CHUNK_ROWS + 2 * a
+                out_sb = held.tile([P, 2, D], F32, name="out_sb")
                 v_ps = tiles["v_ps", k, a]
                 nc.scalar.activation(
-                    out=out_sb[:, 2 * a, :].rearrange("c (q t) -> c q t", t=PACK),
+                    out=out_sb[:, 0, :].rearrange("c (q t) -> c q t", t=PACK),
                     in_=v_ps[:, :, halves[0]].rearrange("c t q -> c q t"),
                     func=ACT.Copy, scale=v_factor[:, r : r + 1],
                 )
                 nc.vector.tensor_scalar_mul(
-                    out=out_sb[:, 2 * a + 1, :].rearrange("c (q t) -> c q t", t=PACK),
+                    out=out_sb[:, 1, :].rearrange("c (q t) -> c q t", t=PACK),
                     in0=v_ps[:, :, halves[1]].rearrange("c t q -> c q t"),
                     scalar1=v_factor[:, r + 1 : r + 2],
                 )
                 nc.sync.dma_start(
-                    out=out_rows[:, r * D : (r + 2) * D],
-                    in_=out_sb[:, 2 * a : 2 * a + 2, :].rearrange("c r f -> c (r f)"),
+                    out=out_rows[:, r * D : (r + 2) * D], in_=out_sb[:].rearrange("c r f -> c (r f)")
                 )
 
         def staged(stage, k, *args):
@@ -406,75 +413,103 @@ def tile_hyperbolicgru_kernel(tc, x, h, Wr, br, Wz, bz, Wh, bh, out):
             sums_of_squares(k, 1)
             norms(k)
 
+        def collect(k):
+            collect_even(k)
+            collect_odd(k)
+
+        def reset(k):
+            reset_h(k)
+            quantise_rh(k)
+
+        both = range(PAIRS)
         sums(0)
         regroup_weights(R, nc.vector.tensor_copy)
         sums(1)
         quantise_weights(R)
-        sums(2)
         logarithms(0)
-        sums_of_squares(3, 0)
+        inverses(0)
+        log_ratio(0)
+        tangents(0)
+        turn_words(0)
+        sums(2)
         logarithms(1)
-        sums_of_squares(3, 1)
-        norms(3)
+        inverses(1)
+        log_ratio(1)
+        collect_even(0)
+        tangents(1)
+        turn_words(1)
+        sums(3)
+        collect_odd(0)
+        logarithms(2)
+        inverses(2)
+        quantise_xh(0)
+        log_ratio(2)
+        gate(R, 0)
+        collect(1)
+        regroup_weights(Z, nc.scalar.copy)
+        tangents(2)
+        turn_words(2)
+        logarithms(3)
+        activate(R, 0)
+        inverses(3)
+        log_ratio(3)
+        quantise_xh(1)
+        h_tangent(0)
+        regroup_weights(N, gpsimd_copy)
+        h_tangent(1)
+        h_tangent(2)
+        tangents(3)
+        gate(R, 1)
+        turn_h(0)
+        collect(2)
+        turn_words(3)
+        h_tangent(3)
+        quantise_weights(Z)
+        gate(Z, 0)
+        reset(0)
+        activate(R, 1)
+        quantise_xh(2)
+        gate(R, 2)
+        quantise_n()
+        place_n()
         nc.vector.tensor_scalar_mul(out=minus_bias[:], in0=bias[:, N, 0:PACK], scalar1=-1.0)
-        for j in range(CHUNKS + 2):
-            staged(inverses, j)
-            staged(collect_even, j - 1)
-            if j == 1:
-                collect_odd(0)
-            if j >= 2:
-                staged(logarithms, j)
-            if j == 2:
-                regroup_weights(Z, nc.scalar.copy)
-            if j == 3:
-                activate(R, 0)
-            if j == 4:
-                activate(R, 1)
-                regroup_weights(N, nc.scalar.copy)
-            staged(log_ratio, j)
-            if j > 2:
-                staged(collect_odd, j - 1)
-            if j == 2:
-                collect_odd(1)
-            if j == 5:
-                activate(Z, 0)
-            if j == 3:
-                quantise_weights(Z)
-            if j == 4:
-                reset_h(0)
-                quantise_rh(0)
-            staged(quantise_xh, j - 1)
-            staged(tangents, j)
-            if j in (1, 2):
-                gate(R, j - 1)
-            staged(turn_words, j)
-            staged(h_tangent, j)
-            if j == 3:
-                turn_h(0)
-                gate(Z, 0)
-            if j == 4:
-                turn_h(1)
-                quantise_n()
-                place_n()
-            if j == 5:
-                keep_h(0)
-        for i in range(1, CHUNKS + 4):
+        activate(Z, 0)
+        collect(3)
+        gate(Z, 1)
+        keep_h(0)
+        turn_h(1)
+        quantise_xh(3)
+        reset(1)
+        activate(R, 2)
+        activate(Z, 1)
+        keep_h(1)
+        turn_h(2)
+        gate(R, 3)
+        for i in range(2, CHUNKS + 2):
             if i + 1 < CHUNKS:
-                gate(R, i + 1)
                 activate(R, i + 1)
             if i < CHUNKS:
                 gate(Z, i)
                 activate(Z, i)
-            staged(reset_h, i)
-            staged(quantise_rh, i)
-            staged(keep_h, i)
+                reset(i)
+                keep_h(i)
             staged(turn_h, i + 1)
-            if i <= CHUNKS:
-                gate(N, i - 1)
-                activate(N, i - 1)
-            staged(take_n, i - 1)
-            staged(turn_back, i - 2)
-            staged(new_norms, i - 2)
-            staged(radius, i - 3)
-            staged(shrink, i - 3)
-            staged(finish, i - 3)
+            gate(N, i - 2)
+            activate(N, i - 2)
+            take_n(i - 2)
+            if i > 2:
+                for a in both:
+                    turn_back(i - 3, a)
+                new_norms(i - 3, both)
+            if i > 3:
+                radius(i - 4, both)
+                finish(i - 4, both)
+        last = CHUNKS - 1
+        for a in both:
+            turn_back(last, a)
+            new_norms(last, [a])
+        radius(last - 1, both)
+        finish(last - 1, both)
+        for a in both:
+            radius(last, [a])
+            finish(last, [a])

@@ -88,10 +88,10 @@ def tile_hyperbolicgru_kernel(tc, x, h, Wr, br, Wz, bz, Wh, bh, out):
         nc.vector.memset(warm[:, 0:1], 1.0)
         nc.scalar.activation(out=warm[:, 1:2], in_=warm[:, 0:1], func=ACT.Ln)
 
-        w_codes = keep.tile([P, GATES, SLOTS * HALF], U32, name="w_codes", align_bytes=64)
-        w_scales = keep.tile([P, GATES, SLOTS * HALF], U8, name="w_scales", align_bytes=64)
-        bd_codes = keep.tile([P, PACK, P], U32, name="bd_codes", align_bytes=64)
-        bd_scales = keep.tile([P, PACK, P], U8, name="bd_scales", align_bytes=64)
+        w_codes = keep.tile([P, 2, SLOTS * HALF], U32, name="w_codes", align_bytes=64)
+        w_scales = keep.tile([P, 2, SLOTS * HALF], U8, name="w_scales", align_bytes=64)
+        bd_codes = keep.tile([P, 2, PACK, P], U32, name="bd_codes", align_bytes=64)
+        bd_scales = keep.tile([P, 2, PACK, P], U8, name="bd_scales", align_bytes=64)
         nh_codes = keep.tile([P, PACK, HALF], U32, name="nh_codes", align_bytes=64)
         nh_scales = keep.tile([P, PACK, HALF], U8, name="nh_scales", align_bytes=64)
         w_grouped = keep.tile([P, GATES, PACK, HALF, PACK], BF16, name="w_grouped", align_bytes=64)
@@ -104,8 +104,6 @@ def tile_hyperbolicgru_kernel(tc, x, h, Wr, br, Wz, bz, Wh, bh, out):
             nc.vector.memset(slot_view(w_codes, g)[:, 0:SLOTS:2, :].bitcast(I32), 0)
             nc.vector.memset(slot_view(w_scales, g)[:, 0:SLOTS:2, :].bitcast(I32), 0)
 
-        nc.vector.memset(w_codes[:, N].bitcast(I32), 0)
-        nc.vector.memset(w_scales[:, N].bitcast(I32), 0)
         nc.vector.memset(bd_codes[:].bitcast(I32), 0)
         nc.vector.memset(bd_scales[:].bitcast(I32), 0)
 
@@ -115,8 +113,8 @@ def tile_hyperbolicgru_kernel(tc, x, h, Wr, br, Wz, bz, Wh, bh, out):
         def gpsimd_copy(out, in_):
             nc.gpsimd.tensor_scalar(out=out, in0=in_, scalar1=1.0, scalar2=0.0, op0=ALU.mult, op1=ALU.add)
 
-        def quantise_weights(g):
-            for t in range(PACK):
+        def quantise_weights(g, tiles_of_gate):
+            for t in tiles_of_gate:
                 at = slice((2 * t + 1) * HALF, (2 * t + 2) * HALF)
                 nc.vector.quantize_mx(
                     out=w_codes[:, g, at].bitcast(FP8X4),
@@ -133,13 +131,11 @@ def tile_hyperbolicgru_kernel(tc, x, h, Wr, br, Wz, bz, Wh, bh, out):
 
         def place_n():
             lower, upper = halves
-            for slots, diag, block in ((w_codes, bd_codes, nh_codes), (w_scales, bd_scales, nh_scales)):
-                nc.vector.tensor_copy(
-                    out=slot_view(slots, N)[lower, 1:SLOTS:2, :].bitcast(I32), in_=block[lower].bitcast(I32)
-                )
-                nc.vector.tensor_copy(out=diag[upper, :, upper].bitcast(I32), in_=block[upper].bitcast(I32))
-                with nc.allow_non_contiguous_dma(reason="a quarter of a tile: runs of 64 columns"):
-                    nc.sync.dma_start(out=diag[lower, :, lower].bitcast(I32), in_=block[upper].bitcast(I32))
+            for diag, block in ((bd_codes, nh_codes), (bd_scales, nh_scales)):
+                for s, own, other in ((0, lower, upper), (1, upper, lower)):
+                    nc.vector.tensor_copy(out=diag[own, s, :, own].bitcast(I32), in_=block[own].bitcast(I32))
+                    with nc.allow_non_contiguous_dma(reason="a quarter of a tile: runs of 64 columns"):
+                        nc.sync.dma_start(out=diag[other, s, :, other].bitcast(I32), in_=block[own].bitcast(I32))
 
         squares = keep.tile([P, 2, ROWS * D], BF16, name="squares")
         sumsq = keep.tile([P, 2, ROWS], F32, name="sumsq")
@@ -175,11 +171,14 @@ def tile_hyperbolicgru_kernel(tc, x, h, Wr, br, Wz, bz, Wh, bh, out):
             nc.scalar.activation(out=ln_plus[:, :, rows], in_=norm[:, :, rows], func=ACT.Ln, bias=1.0, scale=1.0)
             nc.scalar.activation(out=ln_minus[:, :, rows], in_=norm[:, :, rows], func=ACT.Ln, bias=1.0, scale=-1.0)
 
-        def inverses(k):
+        def doubles(k):
             rows = chunk_rows(k)
             nc.vector.tensor_scalar(
                 out=twice[:, :, rows], in0=norm[:, :, rows], scalar1=TINY, scalar2=2.0, op0=ALU.max, op1=ALU.mult
             )
+
+        def inverses(k):
+            rows = chunk_rows(k)
             nc.vector.reciprocal(out=inv_twice[:, :, rows], in_=twice[:, :, rows])
 
         def log_ratio(k):
@@ -259,16 +258,25 @@ def tile_hyperbolicgru_kernel(tc, x, h, Wr, br, Wz, bz, Wh, bh, out):
                 passes.append((w_codes[:, g, at], w_scales[:, g, at], codes[:, s, :], scales[:, s, :]))
             return passes
 
-        def rh_pass(t, k):
-            codes, scales = tiles["rh_mx", k]
-            return [(bd_codes[:, t], bd_scales[:, t], codes[:], scales[:])]
+        def pair_passes(t, k):
+            codes, scales = tiles["xh_mx", k]
+            rh_codes, rh_scales = tiles["rh_mx", k]
+            return [
+                (bd_codes[:, 0, t], bd_scales[:, 0, t], codes[:, 0, :], scales[:, 0, :]),
+                (bd_codes[:, 1, t], bd_scales[:, 1, t], rh_codes[:], rh_scales[:]),
+            ]
+
+        def pair_x(k):
+            lower, upper = halves
+            for tile in tiles["xh_mx", k]:
+                nc.sync.dma_start(out=tile[upper, 0, :].bitcast(I32), in_=tile[lower, 1, :].bitcast(I32))
 
         def gate(g, k):
             for t_pair in range(2):
                 acc = gate_psum.tile([P, 2, COLS], F32, name="acc")
                 for i in range(2):
                     t = 2 * t_pair + i
-                    passes = xh_passes(g, t, k) + (rh_pass(t, k) if g == N else [])
+                    passes = pair_passes(t, k) if g == N else xh_passes(g, t, k)
                     for n, (lhs, lhs_scale, rhs, rhs_scale) in enumerate(passes):
                         nc.tensor.matmul_mx(
                             out=acc[:, i, :], lhsT=lhs.bitcast(FP8X4), lhsT_scale=lhs_scale,
@@ -379,7 +387,13 @@ def tile_hyperbolicgru_kernel(tc, x, h, Wr, br, Wz, bz, Wh, bh, out):
             rows = pair_rows(k, pairs)
             nc.scalar.activation(out=v_tanh[:, rows], in_=v_norm[:, rows], func=ACT.Tanh, scale=-1.0)
             nc.vector.tensor_scalar_max(out=v_floored[:, rows], in0=v_norm[:, rows], scalar1=TINY)
+
+        def invert(k, pairs):
+            rows = pair_rows(k, pairs)
             nc.vector.reciprocal(out=v_inv[:, rows], in_=v_floored[:, rows])
+
+        def shrink(k, pairs):
+            rows = pair_rows(k, pairs)
             nc.vector.scalar_tensor_tensor(
                 out=v_factor[:, rows], in0=v_tanh[:, rows], scalar=-MAX_NORM, in1=v_inv[:, rows],
                 op0=ALU.max, op1=ALU.mult,
@@ -390,16 +404,14 @@ def tile_hyperbolicgru_kernel(tc, x, h, Wr, br, Wz, bz, Wh, bh, out):
                 r = k * CHUNK_ROWS + 2 * a
                 out_sb = held.tile([P, 2, D], F32, name="out_sb")
                 v_ps = tiles["v_ps", k, a]
-                nc.scalar.activation(
-                    out=out_sb[:, 0, :].rearrange("c (q t) -> c q t", t=PACK),
-                    in_=v_ps[:, :, halves[0]].rearrange("c t q -> c q t"),
-                    func=ACT.Copy, scale=v_factor[:, r : r + 1],
-                )
-                nc.vector.tensor_scalar_mul(
-                    out=out_sb[:, 1, :].rearrange("c (q t) -> c q t", t=PACK),
-                    in0=v_ps[:, :, halves[1]].rearrange("c t q -> c q t"),
-                    scalar1=v_factor[:, r + 1 : r + 2],
-                )
+                for i in range(2):
+                    out_view = out_sb[:, i, :].rearrange("c (q t) -> c q t", t=PACK)
+                    in_view = v_ps[:, :, halves[i]].rearrange("c t q -> c q t")
+                    scale = v_factor[:, r + i : r + i + 1]
+                    if i == 0 and k >= CHUNKS // 2:
+                        nc.scalar.activation(out=out_view, in_=in_view, func=ACT.Copy, scale=scale)
+                    else:
+                        nc.vector.tensor_scalar_mul(out=out_view, in0=in_view, scalar1=scale)
                 nc.sync.dma_start(
                     out=out_rows[:, r * D : (r + 2) * D], in_=out_sb[:].rearrange("c r f -> c (r f)")
                 )
@@ -417,72 +429,79 @@ def tile_hyperbolicgru_kernel(tc, x, h, Wr, br, Wz, bz, Wh, bh, out):
             collect_even(k)
             collect_odd(k)
 
-        def reset(k):
-            reset_h(k)
-            quantise_rh(k)
-
         both = range(PAIRS)
         sums(0)
         regroup_weights(R, nc.vector.tensor_copy)
         sums(1)
-        quantise_weights(R)
+        quantise_weights(R, (0, 1))
         logarithms(0)
+        sums(2)
+        doubles(0)
+        quantise_weights(R, (2,))
         inverses(0)
         log_ratio(0)
+        quantise_weights(R, (3,))
         tangents(0)
         turn_words(0)
-        sums(2)
         logarithms(1)
+        doubles(1)
+        sums(3)
         inverses(1)
         log_ratio(1)
         collect_even(0)
         tangents(1)
         turn_words(1)
-        sums(3)
         collect_odd(0)
         logarithms(2)
-        inverses(2)
+        doubles(2)
         quantise_xh(0)
-        log_ratio(2)
+        inverses(2)
         gate(R, 0)
         collect(1)
+        log_ratio(2)
         regroup_weights(Z, nc.scalar.copy)
         tangents(2)
         turn_words(2)
         logarithms(3)
         activate(R, 0)
+        doubles(3)
+        quantise_xh(1)
         inverses(3)
         log_ratio(3)
-        quantise_xh(1)
         h_tangent(0)
         regroup_weights(N, gpsimd_copy)
         h_tangent(1)
         h_tangent(2)
+        collect_even(2)
         tangents(3)
         gate(R, 1)
         turn_h(0)
-        collect(2)
+        collect_odd(2)
         turn_words(3)
         h_tangent(3)
-        quantise_weights(Z)
+        quantise_weights(Z, range(PACK))
         gate(Z, 0)
-        reset(0)
+        pair_x(0)
+        reset_h(0)
         activate(R, 1)
         quantise_xh(2)
         gate(R, 2)
+        quantise_rh(0)
         quantise_n()
-        place_n()
-        nc.vector.tensor_scalar_mul(out=minus_bias[:], in0=bias[:, N, 0:PACK], scalar1=-1.0)
         activate(Z, 0)
         collect(3)
+        place_n()
+        nc.vector.tensor_scalar_mul(out=minus_bias[:], in0=bias[:, N, 0:PACK], scalar1=-1.0)
         gate(Z, 1)
+        pair_x(1)
         keep_h(0)
         turn_h(1)
         quantise_xh(3)
-        reset(1)
+        reset_h(1)
         activate(R, 2)
         activate(Z, 1)
         keep_h(1)
+        quantise_rh(1)
         turn_h(2)
         gate(R, 3)
         for i in range(2, CHUNKS + 2):
@@ -490,9 +509,11 @@ def tile_hyperbolicgru_kernel(tc, x, h, Wr, br, Wz, bz, Wh, bh, out):
                 activate(R, i + 1)
             if i < CHUNKS:
                 gate(Z, i)
+                pair_x(i)
                 activate(Z, i)
-                reset(i)
+                reset_h(i)
                 keep_h(i)
+                quantise_rh(i)
             staged(turn_h, i + 1)
             gate(N, i - 2)
             activate(N, i - 2)
@@ -503,13 +524,23 @@ def tile_hyperbolicgru_kernel(tc, x, h, Wr, br, Wz, bz, Wh, bh, out):
                 new_norms(i - 3, both)
             if i > 3:
                 radius(i - 4, both)
+                invert(i - 4, both)
+                shrink(i - 4, both)
                 finish(i - 4, both)
         last = CHUNKS - 1
         for a in both:
             turn_back(last, a)
             new_norms(last, [a])
         radius(last - 1, both)
-        finish(last - 1, both)
-        for a in both:
-            radius(last, [a])
-            finish(last, [a])
+        invert(last - 1, both)
+        shrink(last - 1, both)
+        finish(last - 1, [0])
+        radius(last, [0])
+        finish(last - 1, [1])
+        invert(last, [0])
+        radius(last, [1])
+        shrink(last, [0])
+        invert(last, [1])
+        finish(last, [0])
+        shrink(last, [1])
+        finish(last, [1])

@@ -338,7 +338,7 @@ def tile_hyperbolicgru_kernel(tc, x, h, Wr, br, Wz, bz, Wh, bh, out):
             tiles["rh_mx", k] = (rh_codes, rh_scales)
 
         def take_n(k):
-            for a, engine in ((0, nc.vector), (1, nc.gpsimd)):
+            for a, engine in ((0, nc.vector), (1, nc.vector)):
                 cols = slice(a * P, (a + 1) * P)
                 taken = held.tile([P, PACK, P], F32, name=f"taken_{a}")
                 engine.tensor_tensor(

@@ -27,7 +27,6 @@ R, Z, N = 0, 1, 2
 SLOTS = 2 * PACK + 1
 TINY = 1e-15
 MAX_NORM = 1.0 - 1e-5
-V_ROWS = 2
 
 FLOPS = 3 * 2 * BATCH * (2 * D) * D
 
@@ -38,6 +37,7 @@ def tile_hyperbolicgru_kernel(tc, x, h, Wr, br, Wz, bz, Wh, bh, out):
         keep = ctx.enter_context(tc.tile_pool(name="keep", bufs=1))
         work = ctx.enter_context(tc.tile_pool(name="work", bufs=2))
         held = ctx.enter_context(tc.tile_pool(name="held", bufs=CHUNKS))
+        outs = ctx.enter_context(tc.tile_pool(name="outs", bufs=CHUNKS * PAIRS))
         turn_psum = ctx.enter_context(tc.psum_pool(name="turn_psum", bufs=4))
         gate_psum = ctx.enter_context(tc.psum_pool(name="gate_psum", bufs=4))
         ctx.enter_context(tc.manual_schedule())
@@ -110,9 +110,6 @@ def tile_hyperbolicgru_kernel(tc, x, h, Wr, br, Wz, bz, Wh, bh, out):
         def regroup_weights(g, copy):
             copy(out=w_grouped[:, g], in_=w_raw[:, g].rearrange("p j (m t) -> p t m j", t=PACK))
 
-        def gpsimd_copy(out, in_):
-            nc.gpsimd.tensor_scalar(out=out, in0=in_, scalar1=1.0, scalar2=0.0, op0=ALU.mult, op1=ALU.add)
-
         def quantise_weights(g, tiles_of_gate):
             for t in tiles_of_gate:
                 at = slice((2 * t + 1) * HALF, (2 * t + 2) * HALF)
@@ -146,21 +143,24 @@ def tile_hyperbolicgru_kernel(tc, x, h, Wr, br, Wz, bz, Wh, bh, out):
         ln_minus = keep.tile([P, 2, ROWS], F32, name="ln_minus")
         ln_diff = keep.tile([P, 2, ROWS], F32, name="ln_diff")
 
-        def sums_of_squares(k, o):
+        def scalar_squares(k, o, pair):
             src = (x_sb, h_sb)[o]
-            for i in range(CHUNK_ROWS):
-                r = k * CHUNK_ROWS + i
+            for i in range(2):
+                r = k * CHUNK_ROWS + 2 * pair + i
                 cols = slice(r * D, (r + 1) * D)
-                if o == 1 and i < V_ROWS:
-                    nc.vector.scalar_tensor_tensor(
-                        out=squares[:, o, cols], in0=src[:, cols], scalar=1.0, in1=src[:, cols],
-                        op0=ALU.mult, op1=ALU.mult, accum_out=sumsq[:, o, r : r + 1],
-                    )
-                else:
-                    nc.scalar.activation(
-                        out=squares[:, o, cols], in_=src[:, cols], func=ACT.Square,
-                        accum_out=sumsq[:, o, r : r + 1],
-                    )
+                nc.scalar.activation(
+                    out=squares[:, o, cols], in_=src[:, cols], func=ACT.Square, accum_out=sumsq[:, o, r : r + 1]
+                )
+
+        def vector_squares(k, o, pair):
+            src = (x_sb, h_sb)[o]
+            for i in range(2):
+                r = k * CHUNK_ROWS + 2 * pair + i
+                cols = slice(r * D, (r + 1) * D)
+                nc.vector.scalar_tensor_tensor(
+                    out=squares[:, o, cols], in0=src[:, cols], scalar=1.0, in1=src[:, cols],
+                    op0=ALU.mult, op1=ALU.mult, accum_out=sumsq[:, o, r : r + 1],
+                )
 
         def norms(k):
             rows = chunk_rows(k)
@@ -234,12 +234,6 @@ def tile_hyperbolicgru_kernel(tc, x, h, Wr, br, Wz, bz, Wh, bh, out):
                 in_=tiles["words_ps", k, s][:].rearrange("p u c -> p c u"),
             )
 
-        def collect_even(k):
-            collect_words(k, 0, nc.vector.tensor_copy)
-
-        def collect_odd(k):
-            collect_words(k, 1, nc.scalar.copy)
-
         def quantise_xh(k):
             xh_codes = held.tile([P, 2, COLS], U32, name="xh_codes", align_bytes=64)
             xh_scales = held.tile([P, 2, COLS], U8, name="xh_scales", align_bytes=64)
@@ -306,27 +300,25 @@ def tile_hyperbolicgru_kernel(tc, x, h, Wr, br, Wz, bz, Wh, bh, out):
                     )
                 tiles["h_ps", k, a] = h_ps
 
-        def reset_h(k):
-            rh_grouped = work.tile([P, COLS, PACK], BF16, name="rh_grouped", align_bytes=64)
-            for a in range(PAIRS):
-                cols = slice(a * P, (a + 1) * P)
-                nc.vector.tensor_tensor(
-                    out=rh_grouped[:, cols, :],
-                    in0=tiles["h_ps", k, a][:].rearrange("p t c -> p c t"),
-                    in1=tiles["r_t", k][:, :, cols].rearrange("p t c -> p c t"),
-                    op=ALU.mult,
-                )
-            tiles["rh_grouped", k] = rh_grouped
+        def reset_h(k, a):
+            if a == 0:
+                tiles["rh_grouped", k] = work.tile([P, COLS, PACK], BF16, name="rh_grouped", align_bytes=64)
+            cols = slice(a * P, (a + 1) * P)
+            nc.vector.tensor_tensor(
+                out=tiles["rh_grouped", k][:, cols, :],
+                in0=tiles["h_ps", k, a][:].rearrange("p t c -> p c t"),
+                in1=tiles["r_t", k][:, :, cols].rearrange("p t c -> p c t"),
+                op=ALU.mult,
+            )
 
-        def keep_h(k):
-            for a in range(PAIRS):
-                cols = slice(a * P, (a + 1) * P)
-                kept = held.tile([P, PACK, P], F32, name=f"kept_{a}")
-                nc.vector.scalar_tensor_tensor(
-                    out=kept[:], in0=tiles["z_t", k][:, :, cols], scalar=1.0, in1=tiles["h_ps", k, a][:],
-                    op0=ALU.subtract, op1=ALU.mult,
-                )
-                tiles["kept", k, a] = kept
+        def keep_h(k, a):
+            cols = slice(a * P, (a + 1) * P)
+            kept = held.tile([P, PACK, P], F32, name=f"kept_{a}")
+            nc.vector.scalar_tensor_tensor(
+                out=kept[:], in0=tiles["z_t", k][:, :, cols], scalar=1.0, in1=tiles["h_ps", k, a][:],
+                op0=ALU.subtract, op1=ALU.mult,
+            )
+            tiles["kept", k, a] = kept
 
         def quantise_rh(k):
             rh_codes = held.tile([P, COLS], U32, name="rh_codes", align_bytes=64)
@@ -337,25 +329,32 @@ def tile_hyperbolicgru_kernel(tc, x, h, Wr, br, Wz, bz, Wh, bh, out):
             )
             tiles["rh_mx", k] = (rh_codes, rh_scales)
 
-        def take_n(k):
-            for a, engine in ((0, nc.vector), (1, nc.vector)):
-                cols = slice(a * P, (a + 1) * P)
-                taken = held.tile([P, PACK, P], F32, name=f"taken_{a}")
-                engine.tensor_tensor(
-                    out=taken[:], in0=tiles["z_t", k][:, :, cols], in1=tiles["n_t", k][:, :, cols], op=ALU.mult
-                )
-                tiles["taken", k, a] = taken
+        def take_n(k, a, engine):
+            cols = slice(a * P, (a + 1) * P)
+            taken = held.tile([P, PACK, P], F32, name=f"taken_{a}")
+            engine.tensor_tensor(
+                out=taken[:], in0=tiles["z_t", k][:, :, cols], in1=tiles["n_t", k][:, :, cols], op=ALU.mult
+            )
+            tiles["taken", k, a] = taken
+
+        def sum_up(k, a):
+            total = held.tile([P, PACK, P], F32, name=f"total_{a}")
+            nc.vector.tensor_tensor(
+                out=total[:], in0=tiles["kept", k, a][:], in1=tiles["taken", k, a][:], op=ALU.add
+            )
+            tiles["parts", k, a] = (total,)
 
         def turn_back(k, a):
             if k < CHUNKS // 2:
                 v_ps = turn_psum.tile([P, PACK, P], F32, name="v_ps", tag="turn")
             else:
                 v_ps = gate_psum.tile([P, PACK, P], F32, name="v_ps", tag="acc")
+            parts = tiles.get(("parts", k, a)) or (tiles["kept", k, a], tiles["taken", k, a])
             for t in range(PACK):
-                for n, part in enumerate(("kept", "taken")):
+                for n, part in enumerate(parts):
                     nc.tensor.matmul(
-                        out=v_ps[:, t, :], lhsT=tiles[part, k, a][:, t, :], rhs=ident[:],
-                        start=(n == 0), stop=(n == 1), is_transpose=True,
+                        out=v_ps[:, t, :], lhsT=part[:, t, :], rhs=ident[:],
+                        start=(n == 0), stop=(n == len(parts) - 1), is_transpose=True,
                     )
             tiles["v_ps", k, a] = v_ps
 
@@ -369,15 +368,16 @@ def tile_hyperbolicgru_kernel(tc, x, h, Wr, br, Wz, bz, Wh, bh, out):
         def pair_rows(k, pairs):
             return slice(k * CHUNK_ROWS + 2 * pairs[0], k * CHUNK_ROWS + 2 * pairs[-1] + 2)
 
+        def scalar_v_squares(k, a):
+            for i in range(2):
+                r = k * CHUNK_ROWS + 2 * a + i
+                nc.scalar.activation(
+                    out=squares[:, 0, r * D : (r + 1) * D].rearrange("c (t q) -> c t q", t=PACK),
+                    in_=tiles["v_ps", k, a][:, :, halves[i]], func=ACT.Square,
+                    accum_out=v_sumsq[:, r : r + 1],
+                )
+
         def new_norms(k, pairs):
-            for a in pairs:
-                for i in range(2):
-                    r = k * CHUNK_ROWS + 2 * a + i
-                    nc.scalar.activation(
-                        out=squares[:, 0, r * D : (r + 1) * D].rearrange("c (t q) -> c t q", t=PACK),
-                        in_=tiles["v_ps", k, a][:, :, halves[i]], func=ACT.Square,
-                        accum_out=v_sumsq[:, r : r + 1],
-                    )
             rows = pair_rows(k, pairs)
             nc.gpsimd.tensor_tensor(
                 out=v_norm[:, rows], in0=v_sumsq[:, rows], in1=half_pow[:, 0, 0 : 2 * len(pairs)], op=ALU.pow
@@ -386,6 +386,9 @@ def tile_hyperbolicgru_kernel(tc, x, h, Wr, br, Wz, bz, Wh, bh, out):
         def radius(k, pairs):
             rows = pair_rows(k, pairs)
             nc.scalar.activation(out=v_tanh[:, rows], in_=v_norm[:, rows], func=ACT.Tanh, scale=-1.0)
+
+        def floor_norms(k, pairs):
+            rows = pair_rows(k, pairs)
             nc.vector.tensor_scalar_max(out=v_floored[:, rows], in0=v_norm[:, rows], scalar1=TINY)
 
         def invert(k, pairs):
@@ -399,148 +402,211 @@ def tile_hyperbolicgru_kernel(tc, x, h, Wr, br, Wz, bz, Wh, bh, out):
                 op0=ALU.max, op1=ALU.mult,
             )
 
-        def finish(k, pairs):
-            for a in pairs:
-                r = k * CHUNK_ROWS + 2 * a
-                out_sb = held.tile([P, 2, D], F32, name="out_sb")
-                v_ps = tiles["v_ps", k, a]
-                for i in range(2):
-                    out_view = out_sb[:, i, :].rearrange("c (q t) -> c q t", t=PACK)
-                    in_view = v_ps[:, :, halves[i]].rearrange("c t q -> c q t")
-                    scale = v_factor[:, r + i : r + i + 1]
-                    if i == 0 and k >= CHUNKS // 2:
-                        nc.scalar.activation(out=out_view, in_=in_view, func=ACT.Copy, scale=scale)
-                    else:
-                        nc.vector.tensor_scalar_mul(out=out_view, in0=in_view, scalar1=scale)
+        def finish_row(k, a, i, engine):
+            r = k * CHUNK_ROWS + 2 * a + i
+            if i == 0:
+                tiles["out_sb", k, a] = outs.tile([P, 2, D], F32, name="out_sb")
+            out_sb = tiles["out_sb", k, a]
+            out_view = out_sb[:, i, :].rearrange("c (q t) -> c q t", t=PACK)
+            in_view = tiles["v_ps", k, a][:, :, halves[i]].rearrange("c t q -> c q t")
+            scale = v_factor[:, r : r + 1]
+            if engine is nc.scalar:
+                nc.scalar.activation(out=out_view, in_=in_view, func=ACT.Copy, scale=scale)
+            else:
+                nc.vector.tensor_scalar_mul(out=out_view, in0=in_view, scalar1=scale)
+            if i == 1:
                 nc.sync.dma_start(
-                    out=out_rows[:, r * D : (r + 2) * D], in_=out_sb[:].rearrange("c r f -> c (r f)")
+                    out=out_rows[:, (r - 1) * D : (r + 1) * D], in_=out_sb[:].rearrange("c r f -> c (r f)")
                 )
 
-        def staged(stage, k, *args):
-            if 0 <= k < CHUNKS:
-                stage(k, *args)
+        def finish(k, a, engine):
+            for i in range(2):
+                finish_row(k, a, i, engine)
 
-        def sums(k):
-            sums_of_squares(k, 0)
-            sums_of_squares(k, 1)
-            norms(k)
+        def negate_bias():
+            nc.vector.tensor_scalar_mul(out=minus_bias[:], in0=bias[:, N, 0:PACK], scalar1=-1.0)
 
-        def collect(k):
-            collect_even(k)
-            collect_odd(k)
-
-        both = range(PAIRS)
-        sums(0)
+        vector_squares(0, 0, 0)
+        scalar_squares(0, 0, 1)
+        vector_squares(0, 1, 0)
+        scalar_squares(0, 1, 1)
+        norms(0)
         regroup_weights(R, nc.vector.tensor_copy)
-        sums(1)
-        quantise_weights(R, (0, 1))
+        scalar_squares(1, 0, 0)
+        scalar_squares(1, 0, 1)
+        vector_squares(1, 1, 0)
+        scalar_squares(1, 1, 1)
+        norms(1)
+        regroup_weights(N, nc.vector.tensor_copy)
+        scalar_squares(2, 0, 0)
+        quantise_weights(R, (0,))
         logarithms(0)
-        sums(2)
+        vector_squares(2, 1, 0)
+        scalar_squares(2, 0, 1)
+        scalar_squares(2, 1, 1)
+        norms(2)
         doubles(0)
+        quantise_weights(R, (1,))
         quantise_weights(R, (2,))
+        quantise_weights(R, (3,))
         inverses(0)
         log_ratio(0)
-        quantise_weights(R, (3,))
+        quantise_n()
         tangents(0)
         turn_words(0)
+        vector_squares(3, 1, 0)
+        scalar_squares(3, 0, 0)
         logarithms(1)
         doubles(1)
-        sums(3)
+        regroup_weights(Z, nc.vector.tensor_copy)
+        scalar_squares(3, 0, 1)
+        scalar_squares(3, 1, 1)
+        norms(3)
         inverses(1)
         log_ratio(1)
-        collect_even(0)
+        collect_words(0, 0, nc.vector.tensor_copy)
         tangents(1)
         turn_words(1)
-        collect_odd(0)
+        collect_words(0, 1, nc.scalar.copy)
         logarithms(2)
         doubles(2)
-        quantise_xh(0)
+        quantise_weights(Z, (0,))
+        quantise_weights(Z, (1,))
         inverses(2)
+        quantise_weights(Z, (2,))
+        quantise_xh(0)
         gate(R, 0)
-        collect(1)
+        collect_words(1, 0, nc.scalar.copy)
         log_ratio(2)
-        regroup_weights(Z, nc.scalar.copy)
+        quantise_weights(Z, (3,))
+        collect_words(1, 1, nc.scalar.copy)
         tangents(2)
         turn_words(2)
-        logarithms(3)
-        activate(R, 0)
-        doubles(3)
-        quantise_xh(1)
-        inverses(3)
-        log_ratio(3)
-        h_tangent(0)
-        regroup_weights(N, gpsimd_copy)
-        h_tangent(1)
-        h_tangent(2)
-        collect_even(2)
-        tangents(3)
-        gate(R, 1)
-        turn_h(0)
-        collect_odd(2)
-        turn_words(3)
-        h_tangent(3)
-        quantise_weights(Z, range(PACK))
         gate(Z, 0)
         pair_x(0)
-        reset_h(0)
-        activate(R, 1)
+        logarithms(3)
+        quantise_xh(1)
+        doubles(3)
+        h_tangent(0)
+        place_n()
+        negate_bias()
+        activate(R, 0)
+        gate(R, 1)
+        collect_words(2, 0, nc.vector.tensor_copy)
+        inverses(3)
+        log_ratio(3)
+        collect_words(2, 1, nc.vector.tensor_copy)
+        tangents(3)
+        turn_h(0)
+        turn_words(3)
+        h_tangent(1)
+        h_tangent(2)
+        h_tangent(3)
+        activate(Z, 0)
         quantise_xh(2)
         gate(R, 2)
-        quantise_rh(0)
-        quantise_n()
-        activate(Z, 0)
-        collect(3)
-        place_n()
-        nc.vector.tensor_scalar_mul(out=minus_bias[:], in0=bias[:, N, 0:PACK], scalar1=-1.0)
+        activate(R, 1)
+        reset_h(0, 0)
+        reset_h(0, 1)
         gate(Z, 1)
         pair_x(1)
-        keep_h(0)
-        turn_h(1)
-        quantise_xh(3)
-        reset_h(1)
+        collect_words(3, 0, nc.scalar.copy)
+        collect_words(3, 1, nc.scalar.copy)
+        keep_h(0, 0)
+        quantise_rh(0)
+        keep_h(0, 1)
         activate(R, 2)
+        turn_h(1)
         activate(Z, 1)
-        keep_h(1)
+        gate(Z, 2)
+        pair_x(2)
+        quantise_xh(3)
+        reset_h(1, 0)
+        reset_h(1, 1)
+        keep_h(1, 0)
         quantise_rh(1)
+        keep_h(1, 1)
         turn_h(2)
+        activate(Z, 2)
         gate(R, 3)
-        for i in range(2, CHUNKS + 2):
-            if i + 1 < CHUNKS:
-                activate(R, i + 1)
-            if i < CHUNKS:
-                gate(Z, i)
-                pair_x(i)
-                activate(Z, i)
-                reset_h(i)
-                keep_h(i)
-                quantise_rh(i)
-            staged(turn_h, i + 1)
-            gate(N, i - 2)
-            activate(N, i - 2)
-            take_n(i - 2)
-            if i > 2:
-                for a in both:
-                    turn_back(i - 3, a)
-                new_norms(i - 3, both)
-            if i > 3:
-                radius(i - 4, both)
-                invert(i - 4, both)
-                shrink(i - 4, both)
-                finish(i - 4, both)
-        last = CHUNKS - 1
-        for a in both:
-            turn_back(last, a)
-            new_norms(last, [a])
-        radius(last - 1, both)
-        invert(last - 1, both)
-        shrink(last - 1, both)
-        finish(last - 1, [0])
-        radius(last, [0])
-        finish(last - 1, [1])
-        invert(last, [0])
-        radius(last, [1])
-        shrink(last, [0])
-        invert(last, [1])
-        finish(last, [0])
-        shrink(last, [1])
-        finish(last, [1])
+        turn_h(3)
+        gate(Z, 3)
+        pair_x(3)
+        activate(R, 3)
+        activate(Z, 3)
+        gate(N, 0)
+        gate(N, 1)
+        reset_h(2, 0)
+        reset_h(2, 1)
+        activate(N, 0)
+        take_n(0, 0, nc.gpsimd)
+        take_n(0, 1, nc.gpsimd)
+        activate(N, 1)
+        keep_h(2, 0)
+        quantise_rh(2)
+        keep_h(2, 1)
+        reset_h(3, 0)
+        reset_h(3, 1)
+        keep_h(3, 0)
+        quantise_rh(3)
+        keep_h(3, 1)
+        gate(N, 2)
+        activate(N, 2)
+        take_n(1, 0, nc.vector)
+        take_n(1, 1, nc.vector)
+        gate(N, 3)
+        activate(N, 3)
+        take_n(2, 0, nc.vector)
+        take_n(2, 1, nc.vector)
+        turn_back(0, 0)
+        turn_back(0, 1)
+        take_n(3, 0, nc.vector)
+        take_n(3, 1, nc.vector)
+        scalar_v_squares(0, 0)
+        scalar_v_squares(0, 1)
+        new_norms(0, [0, 1])
+        turn_back(1, 0)
+        turn_back(1, 1)
+        sum_up(3, 0)
+        sum_up(3, 1)
+        scalar_v_squares(1, 0)
+        scalar_v_squares(1, 1)
+        new_norms(1, [0, 1])
+        turn_back(2, 0)
+        turn_back(2, 1)
+        radius(0, [0, 1])
+        floor_norms(0, [0, 1])
+        invert(0, [0, 1])
+        shrink(0, [0, 1])
+        scalar_v_squares(2, 0)
+        scalar_v_squares(2, 1)
+        new_norms(2, [0, 1])
+        turn_back(3, 0)
+        turn_back(3, 1)
+        finish_row(0, 0, 0, nc.vector)
+        radius(1, [0, 1])
+        floor_norms(1, [0, 1])
+        finish_row(0, 0, 1, nc.vector)
+        invert(1, [0, 1])
+        finish_row(0, 1, 0, nc.vector)
+        shrink(1, [0, 1])
+        finish_row(0, 1, 1, nc.vector)
+        scalar_v_squares(3, 0)
+        scalar_v_squares(3, 1)
+        new_norms(3, [0, 1])
+        finish(1, 0, nc.scalar)
+        finish_row(1, 1, 0, nc.vector)
+        radius(2, [0, 1])
+        floor_norms(2, [0, 1])
+        finish_row(1, 1, 1, nc.vector)
+        invert(2, [0, 1])
+        shrink(2, [0, 1])
+        finish(2, 0, nc.scalar)
+        finish_row(2, 1, 0, nc.vector)
+        radius(3, [0, 1])
+        floor_norms(3, [0, 1])
+        finish_row(2, 1, 1, nc.vector)
+        invert(3, [0, 1])
+        shrink(3, [0, 1])
+        finish(3, 0, nc.scalar)
+        finish(3, 1, nc.vector)

@@ -202,11 +202,11 @@ def tile_hyperbolicgru_kernel(tc, x, h, Wr, br, Wz, bz, Wh, bh, out):
                     )
             tiles["xh_tan", k] = xh_tan
 
-        def h_tangent(k):
+        def h_tangent(k, engine):
             h_tan = held.tile([P, PAIRS, PACK, 2, HALF], F32, name="h_tan")
             for i in range(CHUNK_ROWS):
                 r = k * CHUNK_ROWS + i
-                nc.gpsimd.tensor_scalar(
+                engine.tensor_scalar(
                     out=h_tan[:, i // 2, :, i % 2, :],
                     in0=h_sb[:, r * D : (r + 1) * D].rearrange("c (q t) -> c t q", t=PACK),
                     scalar1=ln_diff[:, 1, r : r + 1], scalar2=inv_twice[:, 1, r : r + 1],
@@ -337,19 +337,12 @@ def tile_hyperbolicgru_kernel(tc, x, h, Wr, br, Wz, bz, Wh, bh, out):
             )
             tiles["taken", k, a] = taken
 
-        def sum_up(k, a):
-            total = held.tile([P, PACK, P], F32, name=f"total_{a}")
-            nc.vector.tensor_tensor(
-                out=total[:], in0=tiles["kept", k, a][:], in1=tiles["taken", k, a][:], op=ALU.add
-            )
-            tiles["parts", k, a] = (total,)
-
         def turn_back(k, a):
             if k < CHUNKS // 2:
                 v_ps = turn_psum.tile([P, PACK, P], F32, name="v_ps", tag="turn")
             else:
                 v_ps = gate_psum.tile([P, PACK, P], F32, name="v_ps", tag="acc")
-            parts = tiles.get(("parts", k, a)) or (tiles["kept", k, a], tiles["taken", k, a])
+            parts = (tiles["kept", k, a], tiles["taken", k, a])
             for t in range(PACK):
                 for n, part in enumerate(parts):
                     nc.tensor.matmul(
@@ -487,7 +480,6 @@ def tile_hyperbolicgru_kernel(tc, x, h, Wr, br, Wz, bz, Wh, bh, out):
         logarithms(3)
         quantise_xh(1)
         doubles(3)
-        h_tangent(0)
         place_n()
         negate_bias()
         activate(R, 0)
@@ -495,13 +487,13 @@ def tile_hyperbolicgru_kernel(tc, x, h, Wr, br, Wz, bz, Wh, bh, out):
         collect_words(2, 0, nc.vector.tensor_copy)
         inverses(3)
         log_ratio(3)
+        h_tangent(0, nc.vector)
         collect_words(2, 1, nc.vector.tensor_copy)
         tangents(3)
         turn_h(0)
         turn_words(3)
-        h_tangent(1)
-        h_tangent(2)
-        h_tangent(3)
+        h_tangent(1, nc.gpsimd)
+        h_tangent(2, nc.gpsimd)
         activate(Z, 0)
         quantise_xh(2)
         gate(R, 2)
@@ -521,6 +513,7 @@ def tile_hyperbolicgru_kernel(tc, x, h, Wr, br, Wz, bz, Wh, bh, out):
         gate(Z, 2)
         pair_x(2)
         quantise_xh(3)
+        h_tangent(3, nc.vector)
         reset_h(1, 0)
         reset_h(1, 1)
         keep_h(1, 0)
@@ -539,8 +532,6 @@ def tile_hyperbolicgru_kernel(tc, x, h, Wr, br, Wz, bz, Wh, bh, out):
         reset_h(2, 0)
         reset_h(2, 1)
         activate(N, 0)
-        take_n(0, 0, nc.gpsimd)
-        take_n(0, 1, nc.gpsimd)
         activate(N, 1)
         keep_h(2, 0)
         quantise_rh(2)
@@ -558,55 +549,55 @@ def tile_hyperbolicgru_kernel(tc, x, h, Wr, br, Wz, bz, Wh, bh, out):
         activate(N, 3)
         take_n(2, 0, nc.vector)
         take_n(2, 1, nc.vector)
-        turn_back(0, 0)
-        turn_back(0, 1)
-        take_n(3, 0, nc.vector)
-        take_n(3, 1, nc.vector)
-        scalar_v_squares(0, 0)
-        scalar_v_squares(0, 1)
-        new_norms(0, [0, 1])
         turn_back(1, 0)
         turn_back(1, 1)
-        sum_up(3, 0)
-        sum_up(3, 1)
+        take_n(0, 0, nc.vector)
+        take_n(0, 1, nc.vector)
+        take_n(3, 0, nc.vector)
+        take_n(3, 1, nc.vector)
         scalar_v_squares(1, 0)
         scalar_v_squares(1, 1)
         new_norms(1, [0, 1])
         turn_back(2, 0)
         turn_back(2, 1)
-        radius(0, [0, 1])
-        floor_norms(0, [0, 1])
-        invert(0, [0, 1])
-        shrink(0, [0, 1])
         scalar_v_squares(2, 0)
         scalar_v_squares(2, 1)
         new_norms(2, [0, 1])
+        turn_back(0, 0)
+        turn_back(0, 1)
+        scalar_v_squares(0, 0)
+        radius(1, [0, 1])
+        scalar_v_squares(0, 1)
+        floor_norms(1, [0, 1])
+        invert(1, [0, 1])
+        shrink(1, [0, 1])
+        new_norms(0, [0, 1])
         turn_back(3, 0)
         turn_back(3, 1)
-        finish_row(0, 0, 0, nc.vector)
-        radius(1, [0, 1])
-        floor_norms(1, [0, 1])
-        finish_row(0, 0, 1, nc.vector)
-        invert(1, [0, 1])
-        finish_row(0, 1, 0, nc.vector)
-        shrink(1, [0, 1])
-        finish_row(0, 1, 1, nc.vector)
+        finish_row(1, 0, 0, nc.vector)
         scalar_v_squares(3, 0)
+        radius(2, [0, 1])
         scalar_v_squares(3, 1)
         new_norms(3, [0, 1])
-        finish(1, 0, nc.scalar)
-        finish_row(1, 1, 0, nc.vector)
-        radius(2, [0, 1])
         floor_norms(2, [0, 1])
-        finish_row(1, 1, 1, nc.vector)
+        finish_row(1, 0, 1, nc.vector)
         invert(2, [0, 1])
+        finish_row(1, 1, 0, nc.vector)
         shrink(2, [0, 1])
+        finish_row(1, 1, 1, nc.vector)
         finish(2, 0, nc.scalar)
+        radius(0, [0, 1])
+        floor_norms(0, [0, 1])
         finish_row(2, 1, 0, nc.vector)
+        invert(0, [0, 1])
+        finish_row(2, 1, 1, nc.vector)
+        shrink(0, [0, 1])
+        finish(0, 0, nc.scalar)
         radius(3, [0, 1])
         floor_norms(3, [0, 1])
-        finish_row(2, 1, 1, nc.vector)
+        finish_row(0, 1, 0, nc.vector)
         invert(3, [0, 1])
+        finish_row(0, 1, 1, nc.vector)
         shrink(3, [0, 1])
         finish(3, 0, nc.scalar)
         finish(3, 1, nc.vector)

@@ -202,16 +202,27 @@ def tile_hyperbolicgru_kernel(tc, x, h, Wr, br, Wz, bz, Wh, bh, out):
                     )
             tiles["xh_tan", k] = xh_tan
 
+        h_factor = keep.tile([P, ROWS], F32, name="h_factor")
+
+        def join_factors(k):
+            rows = chunk_rows(k)
+            nc.vector.tensor_tensor(
+                out=h_factor[:, rows], in0=ln_diff[:, 1, rows], in1=inv_twice[:, 1, rows], op=ALU.mult
+            )
+
         def h_tangent(k, engine):
             h_tan = held.tile([P, PAIRS, PACK, 2, HALF], F32, name="h_tan")
             for i in range(CHUNK_ROWS):
                 r = k * CHUNK_ROWS + i
-                engine.tensor_scalar(
-                    out=h_tan[:, i // 2, :, i % 2, :],
-                    in0=h_sb[:, r * D : (r + 1) * D].rearrange("c (q t) -> c t q", t=PACK),
-                    scalar1=ln_diff[:, 1, r : r + 1], scalar2=inv_twice[:, 1, r : r + 1],
-                    op0=ALU.mult, op1=ALU.mult,
-                )
+                out_view = h_tan[:, i // 2, :, i % 2, :]
+                in_view = h_sb[:, r * D : (r + 1) * D].rearrange("c (q t) -> c t q", t=PACK)
+                if engine is nc.scalar:
+                    nc.scalar.activation(out=out_view, in_=in_view, func=ACT.Copy, scale=h_factor[:, r : r + 1])
+                else:
+                    nc.vector.tensor_scalar(
+                        out=out_view, in0=in_view, scalar1=ln_diff[:, 1, r : r + 1], scalar2=inv_twice[:, 1, r : r + 1],
+                        op0=ALU.mult, op1=ALU.mult,
+                    )
             tiles["h_tan", k] = h_tan
 
         def turn_words(k):
@@ -487,18 +498,19 @@ def tile_hyperbolicgru_kernel(tc, x, h, Wr, br, Wz, bz, Wh, bh, out):
         collect_words(2, 0, nc.vector.tensor_copy)
         inverses(3)
         log_ratio(3)
+        join_factors(2)
         h_tangent(0, nc.vector)
         collect_words(2, 1, nc.vector.tensor_copy)
         tangents(3)
         turn_h(0)
         turn_words(3)
-        h_tangent(1, nc.gpsimd)
-        h_tangent(2, nc.gpsimd)
         activate(Z, 0)
         quantise_xh(2)
         gate(R, 2)
         activate(R, 1)
+        h_tangent(2, nc.scalar)
         reset_h(0, 0)
+        h_tangent(1, nc.vector)
         reset_h(0, 1)
         gate(Z, 1)
         pair_x(1)
@@ -522,9 +534,9 @@ def tile_hyperbolicgru_kernel(tc, x, h, Wr, br, Wz, bz, Wh, bh, out):
         turn_h(2)
         activate(Z, 2)
         gate(R, 3)
-        turn_h(3)
         gate(Z, 3)
         pair_x(3)
+        turn_h(3)
         activate(R, 3)
         activate(Z, 3)
         gate(N, 0)

@@ -26,6 +26,7 @@ GATES = 3
 R, Z, N = 0, 1, 2
 SLOTS = 2 * PACK + 1
 TINY = 1e-15
+SPECK = 1e-17
 MAX_NORM = 1.0 - 1e-5
 
 FLOPS = 3 * 2 * BATCH * (2 * D) * D
@@ -129,10 +130,10 @@ def tile_hyperbolicgru_kernel(tc, x, h, Wr, br, Wz, bz, Wh, bh, out):
         def place_n():
             lower, upper = halves
             for diag, block in ((bd_codes, nh_codes), (bd_scales, nh_scales)):
-                for s, own, other in ((0, lower, upper), (1, upper, lower)):
-                    nc.vector.tensor_copy(out=diag[own, s, :, own].bitcast(I32), in_=block[own].bitcast(I32))
-                    with nc.allow_non_contiguous_dma(reason="a quarter of a tile: runs of 64 columns"):
-                        nc.sync.dma_start(out=diag[other, s, :, other].bitcast(I32), in_=block[own].bitcast(I32))
+                for s, own in ((0, lower), (1, upper)):
+                    for quarter in (lower, upper):
+                        with nc.allow_non_contiguous_dma(reason="a quarter of a tile: runs of 64 columns"):
+                            nc.sync.dma_start(out=diag[quarter, s, :, quarter].bitcast(I32), in_=block[own].bitcast(I32))
 
         squares = keep.tile([P, 2, ROWS * D], BF16, name="squares")
         sumsq = keep.tile([P, 2, ROWS], F32, name="sumsq")
@@ -364,7 +365,6 @@ def tile_hyperbolicgru_kernel(tc, x, h, Wr, br, Wz, bz, Wh, bh, out):
 
         v_sumsq = keep.tile([P, ROWS], F32, name="v_sumsq")
         v_norm = keep.tile([P, ROWS], F32, name="v_norm")
-        v_floored = keep.tile([P, ROWS], F32, name="v_floored")
         v_inv = keep.tile([P, ROWS], F32, name="v_inv")
         v_tanh = keep.tile([P, ROWS], F32, name="v_tanh")
         v_factor = keep.tile([P, ROWS], F32, name="v_factor")
@@ -377,7 +377,7 @@ def tile_hyperbolicgru_kernel(tc, x, h, Wr, br, Wz, bz, Wh, bh, out):
                 r = k * CHUNK_ROWS + 2 * a + i
                 nc.scalar.activation(
                     out=squares[:, 0, r * D : (r + 1) * D].rearrange("c (t q) -> c t q", t=PACK),
-                    in_=tiles["v_ps", k, a][:, :, halves[i]], func=ACT.Square,
+                    in_=tiles["v_ps", k, a][:, :, halves[i]], func=ACT.Square, bias=SPECK,
                     accum_out=v_sumsq[:, r : r + 1],
                 )
 
@@ -391,13 +391,9 @@ def tile_hyperbolicgru_kernel(tc, x, h, Wr, br, Wz, bz, Wh, bh, out):
             rows = pair_rows(k, pairs)
             nc.scalar.activation(out=v_tanh[:, rows], in_=v_norm[:, rows], func=ACT.Tanh, scale=-1.0)
 
-        def floor_norms(k, pairs):
-            rows = pair_rows(k, pairs)
-            nc.vector.tensor_scalar_max(out=v_floored[:, rows], in0=v_norm[:, rows], scalar1=TINY)
-
         def invert(k, pairs):
             rows = pair_rows(k, pairs)
-            nc.vector.reciprocal(out=v_inv[:, rows], in_=v_floored[:, rows])
+            nc.vector.reciprocal(out=v_inv[:, rows], in_=v_norm[:, rows])
 
         def shrink(k, pairs):
             rows = pair_rows(k, pairs)
@@ -428,7 +424,7 @@ def tile_hyperbolicgru_kernel(tc, x, h, Wr, br, Wz, bz, Wh, bh, out):
                 finish_row(k, a, i, engine)
 
         def negate_bias():
-            nc.vector.tensor_scalar_mul(out=minus_bias[:], in0=bias[:, N, 0:PACK], scalar1=-1.0)
+            nc.gpsimd.tensor_scalar_mul(out=minus_bias[:], in0=bias[:, N, 0:PACK], scalar1=-1.0)
 
         vector_squares(0, 0, 0)
         scalar_squares(0, 0, 1)
@@ -580,7 +576,6 @@ def tile_hyperbolicgru_kernel(tc, x, h, Wr, br, Wz, bz, Wh, bh, out):
         scalar_v_squares(0, 0)
         radius(1, [0, 1])
         scalar_v_squares(0, 1)
-        floor_norms(1, [0, 1])
         invert(1, [0, 1])
         shrink(1, [0, 1])
         new_norms(0, [0, 1])
@@ -591,7 +586,6 @@ def tile_hyperbolicgru_kernel(tc, x, h, Wr, br, Wz, bz, Wh, bh, out):
         radius(2, [0, 1])
         scalar_v_squares(3, 1)
         new_norms(3, [0, 1])
-        floor_norms(2, [0, 1])
         finish_row(1, 0, 1, nc.vector)
         invert(2, [0, 1])
         finish_row(1, 1, 0, nc.vector)
@@ -599,14 +593,12 @@ def tile_hyperbolicgru_kernel(tc, x, h, Wr, br, Wz, bz, Wh, bh, out):
         finish_row(1, 1, 1, nc.vector)
         finish(2, 0, nc.scalar)
         radius(0, [0, 1])
-        floor_norms(0, [0, 1])
         finish_row(2, 1, 0, nc.vector)
         invert(0, [0, 1])
         finish_row(2, 1, 1, nc.vector)
         shrink(0, [0, 1])
         finish(0, 0, nc.scalar)
         radius(3, [0, 1])
-        floor_norms(3, [0, 1])
         finish_row(0, 1, 0, nc.vector)
         invert(3, [0, 1])
         finish_row(0, 1, 1, nc.vector)

@@ -317,9 +317,9 @@ def tile_hyperbolicgru_kernel(tc, x, h, Wr, br, Wz, bz, Wh, bh, out):
                 tiles["rh_grouped", k] = work.tile([P, COLS, PACK], BF16, name="rh_grouped", align_bytes=64)
             cols = slice(a * P, (a + 1) * P)
             nc.vector.tensor_tensor(
-                out=tiles["rh_grouped", k][:, cols, :],
-                in0=tiles["h_ps", k, a][:].rearrange("p t c -> p c t"),
-                in1=tiles["r_t", k][:, :, cols].rearrange("p t c -> p c t"),
+                out=tiles["rh_grouped", k][:, cols, :].rearrange("p (b j) t -> p b t j", j=4),
+                in0=tiles["h_ps", k, a][:].rearrange("p t (b j) -> p b t j", j=4),
+                in1=tiles["r_t", k][:, :, cols].rearrange("p t (b j) -> p b t j", j=4),
                 op=ALU.mult,
             )
 

@@ -109,7 +109,10 @@ def tile_hyperbolicgru_kernel(tc, x, h, Wr, br, Wz, bz, Wh, bh, out):
         nc.vector.memset(bd_scales[:].bitcast(I32), 0)
 
         def regroup_weights(g, copy):
-            copy(out=w_grouped[:, g], in_=w_raw[:, g].rearrange("p j (m t) -> p t m j", t=PACK))
+            copy(
+                out=w_grouped[:, g].rearrange("p t (b i) j -> p t b j i", i=4),
+                in_=w_raw[:, g].rearrange("p j (b i t) -> p t b j i", i=4, t=PACK),
+            )
 
         def quantise_weights(g, tiles_of_gate):
             for t in tiles_of_gate:
@@ -464,9 +467,9 @@ def tile_hyperbolicgru_kernel(tc, x, h, Wr, br, Wz, bz, Wh, bh, out):
         norms(3)
         inverses(1)
         log_ratio(1)
-        collect_words(0, 0, nc.vector.tensor_copy)
         tangents(1)
         turn_words(1)
+        collect_words(0, 0, nc.scalar.copy)
         collect_words(0, 1, nc.scalar.copy)
         logarithms(2)
         doubles(2)

from contextlib import ExitStack

import concourse.mybir as mybir
from concourse.masks import make_identity

F32 = mybir.dt.float32
BF16 = mybir.dt.bfloat16
I32 = mybir.dt.int32
U32 = mybir.dt.uint32
U8 = mybir.dt.uint8
FP8X4 = mybir.dt.float8_e4m3fn_x4
ACT = mybir.ActivationFunctionType
ALU = mybir.AluOpType

P = 128
HALF = 64
PACK = 4
BATCH = 2048
D = 256
ROWS = BATCH // P
CHUNKS = 4
CHUNK_ROWS = ROWS // CHUNKS
PAIRS = CHUNK_ROWS // 2
COLS = PAIRS * P
GATES = 3
R, Z, N = 0, 1, 2
SLOTS = 2 * PACK + 1
TINY = 1e-15
SPECK = 1e-17
MAX_NORM = 1.0 - 1e-5

FLOPS = 3 * 2 * BATCH * (2 * D) * D


def tile_hyperbolicgru_kernel(tc, x, h, Wr, br, Wz, bz, Wh, bh, out):
    nc = tc.nc
    with ExitStack() as ctx:
        keep = ctx.enter_context(tc.tile_pool(name="keep", bufs=1))
        work = ctx.enter_context(tc.tile_pool(name="work", bufs=2))
        held = ctx.enter_context(tc.tile_pool(name="held", bufs=CHUNKS))
        outs = ctx.enter_context(tc.tile_pool(name="outs", bufs=CHUNKS * PAIRS))
        turn_psum = ctx.enter_context(tc.psum_pool(name="turn_psum", bufs=4))
        gate_psum = ctx.enter_context(tc.psum_pool(name="gate_psum", bufs=4))
        ctx.enter_context(tc.manual_schedule())

        def chunk_rows(k):
            return slice(k * CHUNK_ROWS, (k + 1) * CHUNK_ROWS)

        halves = (slice(0, HALF), slice(HALF, P))

        x_rows = x.rearrange("(c r) f -> c (r f)", r=ROWS)
        h_rows = h.rearrange("(c r) f -> c (r f)", r=ROWS)
        out_rows = out.rearrange("(c r) f -> c (r f)", r=ROWS)
        x_sb = keep.tile([P, ROWS * D], BF16, name="x_sb")
        h_sb = keep.tile([P, ROWS * D], BF16, name="h_sb")
        w_raw = keep.tile([P, GATES, PACK, D], BF16, name="w_raw")
        bias = keep.tile([P, GATES, 16], BF16, name="bias")

        def load_rows(k):
            cols = slice(k * CHUNK_ROWS * D, (k + 1) * CHUNK_ROWS * D)
            nc.sync.dma_start(out=x_sb[:, cols], in_=x_rows[:, cols])
            nc.sync.dma_start(out=h_sb[:, cols], in_=h_rows[:, cols])

        def load_weights(g, w):
            nc.sync.dma_start(out=w_raw[:, g], in_=w.rearrange("(p j) n -> p j n", j=PACK))

        def load_bias(g, b):
            b_view = b.rearrange("(q t) -> q t", t=PACK)
            for rows in halves:
                nc.sync.dma_start(out=bias[rows, g, 0:PACK], in_=b_view)

        load_rows(0)
        load_weights(R, Wr)
        load_rows(1)
        load_weights(N, Wh)
        load_rows(2)
        load_weights(Z, Wz)
        load_rows(3)
        with nc.allow_non_contiguous_dma(reason="four bias values to a partition"):
            load_bias(R, br)
            load_bias(Z, bz)
            load_bias(N, bh)

        half_pow = keep.tile([P, 2, CHUNK_ROWS], F32, name="half_pow")
        nc.gpsimd.memset(half_pow[:], 0.5)
        ident = keep.tile([P, P], F32, name="ident")
        make_identity(nc, ident[:])
        warm = keep.tile([P, 2], F32, name="warm")
        nc.vector.memset(warm[:, 0:1], 1.0)
        nc.scalar.activation(out=warm[:, 1:2], in_=warm[:, 0:1], func=ACT.Ln)

        w_codes = keep.tile([P, 2, SLOTS * HALF], U32, name="w_codes", align_bytes=64)
        w_scales = keep.tile([P, 2, SLOTS * HALF], U8, name="w_scales", align_bytes=64)
        bd_codes = keep.tile([P, 2, PACK, P], U32, name="bd_codes", align_bytes=64)
        bd_scales = keep.tile([P, 2, PACK, P], U8, name="bd_scales", align_bytes=64)
        nh_codes = keep.tile([P, PACK, HALF], U32, name="nh_codes", align_bytes=64)
        nh_scales = keep.tile([P, PACK, HALF], U8, name="nh_scales", align_bytes=64)
        w_grouped = keep.tile([P, GATES, PACK, HALF, PACK], BF16, name="w_grouped", align_bytes=64)
        minus_bias = keep.tile([P, PACK], F32, name="minus_bias")

        def slot_view(tile, g):
            return tile[:, g].rearrange("p (b c) -> p b c", c=HALF)

        for g in (R, Z):
            nc.vector.memset(slot_view(w_codes, g)[:, 0:SLOTS:2, :].bitcast(I32), 0)
            nc.vector.memset(slot_view(w_scales, g)[:, 0:SLOTS:2, :].bitcast(I32), 0)

        nc.vector.memset(bd_codes[:].bitcast(I32), 0)
        nc.vector.memset(bd_scales[:].bitcast(I32), 0)

        def regroup_weights(g, copy):
            copy(
                out=w_grouped[:, g].rearrange("p t (b i) j -> p t b j i", i=4),
                in_=w_raw[:, g].rearrange("p j (b i t) -> p t b j i", i=4, t=PACK),
            )

        def quantise_weights(g, tiles_of_gate):
            for t in tiles_of_gate:
                at = slice((2 * t + 1) * HALF, (2 * t + 2) * HALF)
                nc.vector.quantize_mx(
                    out=w_codes[:, g, at].bitcast(FP8X4),
                    scales=w_scales[:, g, at],
                    in_=w_grouped[:, g, t].rearrange("p m j -> p (m j)"),
                )

        def quantise_n():
            nc.vector.quantize_mx(
                out=nh_codes[:].rearrange("p t m -> p (t m)").bitcast(FP8X4),
                scales=nh_scales[:].rearrange("p t m -> p (t m)"),
                in_=w_grouped[:, N].rearrange("p t m j -> p (t m j)"),
            )

        def place_n():
            lower, upper = halves
            for diag, block in ((bd_codes, nh_codes), (bd_scales, nh_scales)):
                for s, own in ((0, lower), (1, upper)):
                    for quarter in (lower, upper):
                        with nc.allow_non_contiguous_dma(reason="a quarter of a tile: runs of 64 columns"):
                            nc.sync.dma_start(out=diag[quarter, s, :, quarter].bitcast(I32), in_=block[own].bitcast(I32))

        squares = keep.tile([P, 2, ROWS * D], BF16, name="squares")
        sumsq = keep.tile([P, 2, ROWS], F32, name="sumsq")
        norm = keep.tile([P, 2, ROWS], F32, name="norm")
        twice = keep.tile([P, 2, ROWS], F32, name="twice")
        inv_twice = keep.tile([P, 2, ROWS], F32, name="inv_twice")
        ln_plus = keep.tile([P, 2, ROWS], F32, name="ln_plus")
        ln_minus = keep.tile([P, 2, ROWS], F32, name="ln_minus")
        ln_diff = keep.tile([P, 2, ROWS], F32, name="ln_diff")

        def scalar_squares(k, o, pair):
            src = (x_sb, h_sb)[o]
            for i in range(2):
                r = k * CHUNK_ROWS + 2 * pair + i
                cols = slice(r * D, (r + 1) * D)
                nc.scalar.activation(
                    out=squares[:, o, cols], in_=src[:, cols], func=ACT.Square, accum_out=sumsq[:, o, r : r + 1]
                )

        def vector_squares(k, o, pair):
            src = (x_sb, h_sb)[o]
            for i in range(2):
                r = k * CHUNK_ROWS + 2 * pair + i
                cols = slice(r * D, (r + 1) * D)
                nc.vector.scalar_tensor_tensor(
                    out=squares[:, o, cols], in0=src[:, cols], scalar=1.0, in1=src[:, cols],
                    op0=ALU.mult, op1=ALU.mult, accum_out=sumsq[:, o, r : r + 1],
                )

        def norms(k):
            rows = chunk_rows(k)
            nc.gpsimd.tensor_tensor(out=norm[:, :, rows], in0=sumsq[:, :, rows], in1=half_pow[:], op=ALU.pow)

        def logarithms(k):
            rows = chunk_rows(k)
            nc.scalar.activation(out=ln_plus[:, :, rows], in_=norm[:, :, rows], func=ACT.Ln, bias=1.0, scale=1.0)
            nc.scalar.activation(out=ln_minus[:, :, rows], in_=norm[:, :, rows], func=ACT.Ln, bias=1.0, scale=-1.0)

        def doubles(k):
            rows = chunk_rows(k)
            nc.vector.tensor_scalar(
                out=twice[:, :, rows], in0=norm[:, :, rows], scalar1=TINY, scalar2=2.0, op0=ALU.max, op1=ALU.mult
            )

        def inverses(k):
            rows = chunk_rows(k)
            nc.vector.reciprocal(out=inv_twice[:, :, rows], in_=twice[:, :, rows])

        def log_ratio(k):
            rows = chunk_rows(k)
            nc.vector.tensor_tensor(
                out=ln_diff[:, :, rows], in0=ln_plus[:, :, rows], in1=ln_minus[:, :, rows], op=ALU.subtract
            )

        tiles = {}

        def tangents(k):
            xh_tan = work.tile([P, CHUNK_ROWS, 2, 2, HALF, 2], BF16, name="xh_tan")
            for i in range(CHUNK_ROWS):
                r = k * CHUNK_ROWS + i
                for o, src in enumerate((x_sb, h_sb)):
                    nc.vector.tensor_scalar(
                        out=xh_tan[:, i, :, o],
                        in0=src[:, r * D : (r + 1) * D].rearrange("c (p u e) -> c u p e", u=2, e=2),
                        scalar1=ln_diff[:, o, r : r + 1], scalar2=inv_twice[:, o, r : r + 1],
                        op0=ALU.mult, op1=ALU.mult,
                    )
            tiles["xh_tan", k] = xh_tan

        h_factor = keep.tile([P, ROWS], F32, name="h_factor")

        def join_factors(k):
            rows = chunk_rows(k)
            nc.vector.tensor_tensor(
                out=h_factor[:, rows], in0=ln_diff[:, 1, rows], in1=inv_twice[:, 1, rows], op=ALU.mult
            )

        def h_tangent(k, engine):
            h_tan = held.tile([P, PAIRS, PACK, 2, HALF], F32, name="h_tan")
            for i in range(CHUNK_ROWS):
                r = k * CHUNK_ROWS + i
                out_view = h_tan[:, i // 2, :, i % 2, :]
                in_view = h_sb[:, r * D : (r + 1) * D].rearrange("c (q t) -> c t q", t=PACK)
                if engine is nc.scalar:
                    nc.scalar.activation(out=out_view, in_=in_view, func=ACT.Copy, scale=h_factor[:, r : r + 1])
                else:
                    nc.vector.tensor_scalar(
                        out=out_view, in0=in_view, scalar1=ln_diff[:, 1, r : r + 1], scalar2=inv_twice[:, 1, r : r + 1],
                        op0=ALU.mult, op1=ALU.mult,
                    )
            tiles["h_tan", k] = h_tan

        def turn_words(k):
            words = tiles["xh_tan", k][:].rearrange("c i u o p e -> c (i u o p e)").bitcast(F32)
            for s in range(2):
                words_ps = turn_psum.tile([P, 2, COLS], F32, name="words_ps", tag="turn")
                for a in range(PAIRS):
                    for u in range(2):
                        at = ((2 * a + s) * 2 + u) * P
                        nc.tensor.transpose(
                            out=words_ps[:, u, a * P : (a + 1) * P], in_=words[:, at : at + P], identity=ident[:]
                        )
                tiles["words_ps", k, s] = words_ps

        def collect_words(k, s, copy):
            if s == 0:
                tiles["grouped", k] = work.tile([P, 2, COLS, PACK], BF16, name="grouped", align_bytes=64)
            copy(
                out=tiles["grouped", k][:, s].rearrange("p c t -> p (c t)").bitcast(F32).rearrange("p (c u) -> p c u", u=2),
                in_=tiles["words_ps", k, s][:].rearrange("p u c -> p c u"),
            )

        def quantise_xh(k):
            xh_codes = held.tile([P, 2, COLS], U32, name="xh_codes", align_bytes=64)
            xh_scales = held.tile([P, 2, COLS], U8, name="xh_scales", align_bytes=64)
            nc.vector.quantize_mx(
                out=xh_codes[:].rearrange("p s c -> p (s c)").bitcast(FP8X4),
                scales=xh_scales[:].rearrange("p s c -> p (s c)"),
                in_=tiles["grouped", k][:].rearrange("p s c t -> p (s c t)"),
            )
            tiles["xh_mx", k] = (xh_codes, xh_scales)

        def xh_passes(g, t, k):
            codes, scales = tiles["xh_mx", k]
            passes = []
            for s in range(2):
                at = slice((2 * t + 1 - s) * HALF, (2 * t + 3 - s) * HALF)
                passes.append((w_codes[:, g, at], w_scales[:, g, at], codes[:, s, :], scales[:, s, :]))
            return passes

        def pair_passes(t, k):
            codes, scales = tiles["xh_mx", k]
            rh_codes, rh_scales = tiles["rh_mx", k]
            return [
                (bd_codes[:, 0, t], bd_scales[:, 0, t], codes[:, 0, :], scales[:, 0, :]),
                (bd_codes[:, 1, t], bd_scales[:, 1, t], rh_codes[:], rh_scales[:]),
            ]

        def pair_x(k):
            lower, upper = halves
            for tile in tiles["xh_mx", k]:
                nc.sync.dma_start(out=tile[upper, 0, :].bitcast(I32), in_=tile[lower, 1, :].bitcast(I32))

        def gate(g, k):
            for t_pair in range(2):
                acc = gate_psum.tile([P, 2, COLS], F32, name="acc")
                for i in range(2):
                    t = 2 * t_pair + i
                    passes = pair_passes(t, k) if g == N else xh_passes(g, t, k)
                    for n, (lhs, lhs_scale, rhs, rhs_scale) in enumerate(passes):
                        nc.tensor.matmul_mx(
                            out=acc[:, i, :], lhsT=lhs.bitcast(FP8X4), lhsT_scale=lhs_scale,
                            rhs=rhs.bitcast(FP8X4), rhs_scale=rhs_scale,
                            start=(n == 0), stop=(n == len(passes) - 1),
                        )
                tiles["acc", g, k, t_pair] = acc

        def activate(g, k):
            result = held.tile([P, PACK, COLS], F32, name="gate_" + "rzn"[g])
            for t in range(PACK):
                nc.scalar.activation(
                    out=result[:, t, :], in_=tiles["acc", g, k, t // 2][:, t % 2, :],
                    func=ACT.Tanh if g == N else ACT.Sigmoid,
                    bias=minus_bias[:, t : t + 1] if g == N else bias[:, g, t : t + 1],
                    scale=-1.0 if g == N else 1.0,
                )
            tiles["rzn"[g] + "_t", k] = result

        def turn_h(k):
            for a in range(PAIRS):
                h_ps = turn_psum.tile([P, PACK, P], F32, name="h_ps", tag="turn")
                for t in range(PACK):
                    nc.tensor.transpose(
                        out=h_ps[:, t, :], in_=tiles["h_tan", k][:, a, t].rearrange("c r q -> c (r q)"),
                        identity=ident[:],
                    )
                tiles["h_ps", k, a] = h_ps

        def reset_h(k, a):
            if a == 0:
                tiles["rh_grouped", k] = work.tile([P, COLS, PACK], BF16, name="rh_grouped", align_bytes=64)
            cols = slice(a * P, (a + 1) * P)
            nc.vector.tensor_tensor(
                out=tiles["rh_grouped", k][:, cols, :].rearrange("p (b j) t -> p b t j", j=4),
                in0=tiles["h_ps", k, a][:].rearrange("p t (b j) -> p b t j", j=4),
                in1=tiles["r_t", k][:, :, cols].rearrange("p t (b j) -> p b t j", j=4),
                op=ALU.mult,
            )

        def keep_h(k, a):
            cols = slice(a * P, (a + 1) * P)
            kept = held.tile([P, PACK, P], F32, name=f"kept_{a}")
            nc.vector.scalar_tensor_tensor(
                out=kept[:], in0=tiles["z_t", k][:, :, cols], scalar=1.0, in1=tiles["h_ps", k, a][:],
                op0=ALU.subtract, op1=ALU.mult,
            )
            tiles["kept", k, a] = kept

        def quantise_rh(k):
            rh_codes = held.tile([P, COLS], U32, name="rh_codes", align_bytes=64)
            rh_scales = held.tile([P, COLS], U8, name="rh_scales", align_bytes=64)
            nc.vector.quantize_mx(
                out=rh_codes[:].bitcast(FP8X4), scales=rh_scales[:],
                in_=tiles["rh_grouped", k][:].rearrange("p c t -> p (c t)"),
            )
            tiles["rh_mx", k] = (rh_codes, rh_scales)

        def take_n(k, a, engine):
            cols = slice(a * P, (a + 1) * P)
            taken = held.tile([P, PACK, P], F32, name=f"taken_{a}")
            engine.tensor_tensor(
                out=taken[:], in0=tiles["z_t", k][:, :, cols], in1=tiles["n_t", k][:, :, cols], op=ALU.mult
            )
            tiles["taken", k, a] = taken

        def turn_back(k, a):
            if k < CHUNKS // 2:
                v_ps = turn_psum.tile([P, PACK, P], F32, name="v_ps", tag="turn")
            else:
                v_ps = gate_psum.tile([P, PACK, P], F32, name="v_ps", tag="acc")
            parts = (tiles["kept", k, a], tiles["taken", k, a])
            for t in range(PACK):
                for n, part in enumerate(parts):
                    nc.tensor.matmul(
                        out=v_ps[:, t, :], lhsT=part[:, t, :], rhs=ident[:],
                        start=(n == 0), stop=(n == len(parts) - 1), is_transpose=True,
                    )
            tiles["v_ps", k, a] = v_ps

        v_sumsq = keep.tile([P, ROWS], F32, name="v_sumsq")
        v_norm = keep.tile([P, ROWS], F32, name="v_norm")
        v_inv = keep.tile([P, ROWS], F32, name="v_inv")
        v_tanh = keep.tile([P, ROWS], F32, name="v_tanh")
        v_factor = keep.tile([P, ROWS], F32, name="v_factor")

        def pair_rows(k, pairs):
            return slice(k * CHUNK_ROWS + 2 * pairs[0], k * CHUNK_ROWS + 2 * pairs[-1] + 2)

        def scalar_v_squares(k, a):
            for i in range(2):
                r = k * CHUNK_ROWS + 2 * a + i
                nc.scalar.activation(
                    out=squares[:, 0, r * D : (r + 1) * D].rearrange("c (t q) -> c t q", t=PACK),
                    in_=tiles["v_ps", k, a][:, :, halves[i]], func=ACT.Square, bias=SPECK,
                    accum_out=v_sumsq[:, r : r + 1],
                )

        def new_norms(k, pairs):
            rows = pair_rows(k, pairs)
            nc.gpsimd.tensor_tensor(
                out=v_norm[:, rows], in0=v_sumsq[:, rows], in1=half_pow[:, 0, 0 : 2 * len(pairs)], op=ALU.pow
            )

        def radius(k, pairs):
            rows = pair_rows(k, pairs)
            nc.scalar.activation(out=v_tanh[:, rows], in_=v_norm[:, rows], func=ACT.Tanh, scale=-1.0)

        def invert(k, pairs):
            rows = pair_rows(k, pairs)
            nc.vector.reciprocal(out=v_inv[:, rows], in_=v_norm[:, rows])

        def shrink(k, pairs):
            rows = pair_rows(k, pairs)
            nc.vector.scalar_tensor_tensor(
                out=v_factor[:, rows], in0=v_tanh[:, rows], scalar=-MAX_NORM, in1=v_inv[:, rows],
                op0=ALU.max, op1=ALU.mult,
            )

        def finish_row(k, a, i, engine):
            r = k * CHUNK_ROWS + 2 * a + i
            if i == 0:
                tiles["out_sb", k, a] = outs.tile([P, 2, D], F32, name="out_sb")
            out_sb = tiles["out_sb", k, a]
            out_view = out_sb[:, i, :].rearrange("c (q t) -> c q t", t=PACK)
            in_view = tiles["v_ps", k, a][:, :, halves[i]].rearrange("c t q -> c q t")
            scale = v_factor[:, r : r + 1]
            if engine is nc.scalar:
                nc.scalar.activation(out=out_view, in_=in_view, func=ACT.Copy, scale=scale)
            else:
                nc.vector.tensor_scalar_mul(out=out_view, in0=in_view, scalar1=scale)
            if i == 1:
                nc.sync.dma_start(
                    out=out_rows[:, (r - 1) * D : (r + 1) * D], in_=out_sb[:].rearrange("c r f -> c (r f)")
                )

        def finish(k, a, engine):
            for i in range(2):
                finish_row(k, a, i, engine)

        def negate_bias():
            nc.gpsimd.tensor_scalar_mul(out=minus_bias[:], in0=bias[:, N, 0:PACK], scalar1=-1.0)

        vector_squares(0, 0, 0)
        scalar_squares(0, 0, 1)
        vector_squares(0, 1, 0)
        scalar_squares(0, 1, 1)
        norms(0)
        regroup_weights(R, nc.vector.tensor_copy)
        scalar_squares(1, 0, 0)
        scalar_squares(1, 0, 1)
        vector_squares(1, 1, 0)
        scalar_squares(1, 1, 1)
        norms(1)
        regroup_weights(N, nc.vector.tensor_copy)
        scalar_squares(2, 0, 0)
        quantise_weights(R, (0,))
        logarithms(0)
        vector_squares(2, 1, 0)
        scalar_squares(2, 0, 1)
        scalar_squares(2, 1, 1)
        norms(2)
        doubles(0)
        quantise_weights(R, (1,))
        quantise_weights(R, (2,))
        quantise_weights(R, (3,))
        inverses(0)
        log_ratio(0)
        quantise_n()
        tangents(0)
        turn_words(0)
        vector_squares(3, 1, 0)
        scalar_squares(3, 0, 0)
        logarithms(1)
        doubles(1)
        regroup_weights(Z, nc.vector.tensor_copy)
        scalar_squares(3, 0, 1)
        scalar_squares(3, 1, 1)
        norms(3)
        inverses(1)
        log_ratio(1)
        tangents(1)
        turn_words(1)
        collect_words(0, 0, nc.scalar.copy)
        collect_words(0, 1, nc.scalar.copy)
        logarithms(2)
        doubles(2)
        quantise_weights(Z, (0,))
        quantise_weights(Z, (1,))
        inverses(2)
        quantise_weights(Z, (2,))
        quantise_xh(0)
        gate(R, 0)
        collect_words(1, 0, nc.scalar.copy)
        log_ratio(2)
        quantise_weights(Z, (3,))
        collect_words(1, 1, nc.scalar.copy)
        tangents(2)
        turn_words(2)
        gate(Z, 0)
        pair_x(0)
        logarithms(3)
        quantise_xh(1)
        doubles(3)
        place_n()
        negate_bias()
        activate(R, 0)
        gate(R, 1)
        collect_words(2, 0, nc.vector.tensor_copy)
        inverses(3)
        log_ratio(3)
        join_factors(2)
        h_tangent(0, nc.vector)
        collect_words(2, 1, nc.vector.tensor_copy)
        tangents(3)
        turn_h(0)
        turn_words(3)
        activate(Z, 0)
        quantise_xh(2)
        gate(R, 2)
        activate(R, 1)
        h_tangent(2, nc.scalar)
        reset_h(0, 0)
        h_tangent(1, nc.vector)
        reset_h(0, 1)
        gate(Z, 1)
        pair_x(1)
        collect_words(3, 0, nc.scalar.copy)
        collect_words(3, 1, nc.scalar.copy)
        keep_h(0, 0)
        quantise_rh(0)
        keep_h(0, 1)
        activate(R, 2)
        turn_h(1)
        activate(Z, 1)
        gate(Z, 2)
        pair_x(2)
        quantise_xh(3)
        h_tangent(3, nc.vector)
        reset_h(1, 0)
        reset_h(1, 1)
        keep_h(1, 0)
        quantise_rh(1)
        keep_h(1, 1)
        turn_h(2)
        activate(Z, 2)
        gate(R, 3)
        gate(Z, 3)
        pair_x(3)
        turn_h(3)
        activate(R, 3)
        activate(Z, 3)
        gate(N, 0)
        gate(N, 1)
        reset_h(2, 0)
        reset_h(2, 1)
        activate(N, 0)
        activate(N, 1)
        keep_h(2, 0)
        quantise_rh(2)
        keep_h(2, 1)
        reset_h(3, 0)
        reset_h(3, 1)
        keep_h(3, 0)
        quantise_rh(3)
        keep_h(3, 1)
        gate(N, 2)
        activate(N, 2)
        take_n(1, 0, nc.vector)
        take_n(1, 1, nc.vector)
        gate(N, 3)
        activate(N, 3)
        take_n(2, 0, nc.vector)
        take_n(2, 1, nc.vector)
        turn_back(1, 0)
        turn_back(1, 1)
        take_n(0, 0, nc.vector)
        take_n(0, 1, nc.vector)
        take_n(3, 0, nc.vector)
        take_n(3, 1, nc.vector)
        scalar_v_squares(1, 0)
        scalar_v_squares(1, 1)
        new_norms(1, [0, 1])
        turn_back(2, 0)
        turn_back(2, 1)
        scalar_v_squares(2, 0)
        scalar_v_squares(2, 1)
        new_norms(2, [0, 1])
        turn_back(0, 0)
        turn_back(0, 1)
        scalar_v_squares(0, 0)
        radius(1, [0, 1])
        scalar_v_squares(0, 1)
        invert(1, [0, 1])
        shrink(1, [0, 1])
        new_norms(0, [0, 1])
        turn_back(3, 0)
        turn_back(3, 1)
        finish_row(1, 0, 0, nc.vector)
        scalar_v_squares(3, 0)
        radius(2, [0, 1])
        scalar_v_squares(3, 1)
        new_norms(3, [0, 1])
        finish_row(1, 0, 1, nc.vector)
        invert(2, [0, 1])
        finish_row(1, 1, 0, nc.vector)
        shrink(2, [0, 1])
        finish_row(1, 1, 1, nc.vector)
        finish(2, 0, nc.scalar)
        radius(0, [0, 1])
        finish_row(2, 1, 0, nc.vector)
        invert(0, [0, 1])
        finish_row(2, 1, 1, nc.vector)
        shrink(0, [0, 1])
        finish(0, 0, nc.scalar)
        radius(3, [0, 1])
        finish_row(0, 1, 0, nc.vector)
        invert(3, [0, 1])
        finish_row(0, 1, 1, nc.vector)
        shrink(3, [0, 1])
        finish(3, 0, nc.scalar)
        finish(3, 1, nc.vector)
